import numpy as np
import ml_dtypes


def mxq(x, axis, fmt="e4m3"):
    dtype, down = {"e4m3": (ml_dtypes.float8_e4m3fn, 7), "e5m2": (ml_dtypes.float8_e5m2, 14)}[fmt]
    v = np.moveaxis(np.asarray(x, np.float32).astype(ml_dtypes.bfloat16).astype(np.float64), axis, -1)
    blocks = v.reshape(v.shape[:-1] + (-1, 32))
    amax = np.abs(blocks).max(-1, keepdims=True)
    byte = np.maximum(np.where(amax > 0, np.frexp(amax)[1] - 1 + 127, 0) - down, 1)
    scale = np.exp2(byte - 127.0)
    codes = (blocks / scale).astype(np.float32).astype(dtype).astype(np.float64)
    return np.moveaxis((codes * scale).reshape(v.shape), -1, axis)


WIDE = False


def mx_kscale(k):
    if not WIDE:
        return np.ones(k)
    levels = np.array([10, -10, 5, -5, 0])
    if k % 512:
        return np.exp2(np.random.permutation(np.resize(levels, k // 32))).repeat(32)
    a = np.empty((k // 512, 16))
    for p in range(k // 512):
        a[p, :8] = np.random.permutation(np.resize(levels, 8))
        for g in range(8):
            far = levels[np.abs(levels - a[p, g]) >= 10]
            a[p, g + 8] = far[np.random.randint(len(far))]
    return np.exp2(a.ravel()).repeat(32)


BF16 = ml_dtypes.bfloat16


def bf(x):
    return np.asarray(x, np.float32).astype(BF16)


def f64(x):
    return np.asarray(x).astype(np.float64)


E2M1 = np.array([0.0, 0.5, 1.0, 1.5, 2.0, 3.0, 4.0, 6.0, -0.0, -0.5, -1.0, -1.5, -2.0, -3.0, -4.0, -6.0])


def pack_weight(w, fmt):
    k, n = w.shape
    w = f64(bf(w)).reshape(k // 32, 32, n)
    amax = np.abs(w).max(1)
    if fmt == "e4m3":
        byte = np.frexp(amax)[1] - 1 + 127 - 7
    else:
        mant, ex = np.frexp(amax / 6.0)
        byte = np.where(mant > 0.5, ex, ex - 1) + 127
    byte = np.clip(np.where(amax > 0, byte, 1), 1, 254)
    scaled = (w * np.exp2(127.0 - byte)[:, None, :]).reshape(k, n).astype(np.float32)
    by_word = np.ascontiguousarray(scaled.reshape(k // 512, 128, 4, n).transpose(0, 1, 3, 2))
    if fmt == "e4m3":
        words = by_word.astype(ml_dtypes.float8_e4m3fn).view(np.uint8)
    else:
        c = by_word.astype(ml_dtypes.float4_e2m1fn).view(np.uint8) & 0xF
        words = c[..., 0::2] | (c[..., 1::2] << 4)
    return np.ascontiguousarray(words), np.ascontiguousarray(byte.astype(np.uint8).reshape(k // 512, 16, n))


def unpack_weight(words, scales, fmt):
    g, p, n, _ = words.shape
    if fmt == "e4m3":
        vals = np.ascontiguousarray(words).view(ml_dtypes.float8_e4m3fn).astype(np.float64)
    else:
        nib = np.empty((g, p, n, 4), np.uint8)
        nib[..., 0::2] = words & 0xF
        nib[..., 1::2] = words >> 4
        vals = E2M1[nib]
    vals = vals * np.repeat(np.exp2(scales.astype(np.float64) - 127.0), 8, axis=1)[..., None]
    return vals.transpose(0, 1, 3, 2).reshape(g * 512, n)


B, L, A, W = 128, 512, 2048, 8
EPS = 1e-8


def sigmoid(v):
    return 1.0 / (1.0 + np.exp(-v))


def draw0():
    s, t = mx_kscale(L), mx_kscale(A)
    z_current = bf(np.random.standard_normal((B, L)) * s)
    z_window = bf(np.random.standard_normal((W, B, L)) * s)
    Wq_words, Wq_scales = pack_weight((np.random.standard_normal((A, L)) / np.sqrt(L) / s).T, "e4m3")
    Wk_words, Wk_scales = pack_weight((np.random.standard_normal((A, L)) / np.sqrt(L) / s).T, "e4m3")
    Wv_words, Wv_scales = pack_weight((np.random.standard_normal((A, L)) / np.sqrt(L) / s * t[:, None]).T, "e4m3")
    Wo_words, Wo_scales = pack_weight((np.random.standard_normal((L, A)) * 2.0 / np.sqrt(A) / t).T, "e4m3")
    return {
        "z_current": z_current,
        "z_window": z_window,
        "Wq_words": Wq_words,
        "Wq_scales": Wq_scales,
        "Wk_words": Wk_words,
        "Wk_scales": Wk_scales,
        "Wv_words": Wv_words,
        "Wv_scales": Wv_scales,
        "Wo_words": Wo_words,
        "Wo_scales": Wo_scales,
    }


def core(z_current, z_window, Wq_words, Wq_scales, Wk_words, Wk_scales, Wv_words, Wv_scales, Wo_words, Wo_scales):
    sig_q = sigmoid(mxq(f64(z_current), 1, "e4m3") @ unpack_weight(Wq_words, Wq_scales, "e4m3"))
    zw = mxq(f64(z_window), 2, "e4m3")
    k = zw @ unpack_weight(Wk_words, Wk_scales, "e4m3")
    v = zw @ unpack_weight(Wv_words, Wv_scales, "e4m3")
    m = k.max(axis=(1, 2), keepdims=True)
    e = np.exp(k - m)
    num = (e * v).sum(0)
    den = EPS + e.sum(0)
    h = sig_q * (num / den)
    return mxq(h, 1, "e4m3") @ unpack_weight(Wo_words, Wo_scales, "e4m3")


def e4m3fn_bytes(y):
    return np.clip(np.asarray(y, np.float64), -448.0, 448.0).astype(np.float32).astype(ml_dtypes.float8_e4m3fn).view(np.uint8)


def e4m3fn_values(b):
    return np.asarray(b, np.uint8).view(ml_dtypes.float8_e4m3fn).astype(np.float64)


def setup_inputs():
    d = draw0()
    x0 = np.asarray(d['z_window']).astype(np.float64)
    s = (np.max(np.abs(x0), axis=(0, 1), keepdims=True) / 448.0).astype(np.float32)
    out = {}
    for k, v in d.items():
        if k == 'z_window':
            out['z_window_bytes'] = e4m3fn_bytes(x0 / s.astype(np.float64))
            out['z_window_scale'] = s
        else:
            out[k] = v
    return out


def reference(z_current, z_window_bytes, z_window_scale, Wq_words, Wq_scales, Wk_words, Wk_scales, Wv_words, Wv_scales, Wo_words, Wo_scales):
    return core(z_current, e4m3fn_values(z_window_bytes) * z_window_scale.astype(np.float64), Wq_words, Wq_scales, Wk_words, Wk_scales, Wv_words, Wv_scales, Wo_words, Wo_scales)

@@ -1,0 +1,429 @@
+from contextlib import ExitStack
+
+import concourse.mybir as mybir
+from concourse.masks import make_identity
+
+F32 = mybir.dt.float32
+BF16 = mybir.dt.bfloat16
+I32 = mybir.dt.int32
+U32 = mybir.dt.uint32
+U8 = mybir.dt.uint8
+FP8 = mybir.dt.float8_e4m3fn
+FP8X4 = mybir.dt.float8_e4m3fn_x4
+ACT = mybir.ActivationFunctionType
+ALU = mybir.AluOpType
+AX = mybir.AxisListType
+
+P = 128
+B, L, A, W = 128, 512, 2048, 8
+G = A // 512
+EPS = 1e-8
+FLOPS = 2 * B * L * A * (1 + 2 * W) + 2 * B * A * L
+PE_DEN = (7,)
+G_UNITS = ()
+LOOK = 2
+
+
+def tile_aftblock_pa_w8_kernel(tc, z_current, z_window_bytes, z_window_scale, Wq_words, Wq_scales, Wk_words, Wk_scales, Wv_words, Wv_scales, Wo_words, Wo_scales, out):
+    nc = tc.nc
+    with ExitStack() as ctx:
+        keep = ctx.enter_context(tc.tile_pool(name="keep", bufs=1))
+        work = ctx.enter_context(tc.tile_pool(name="work", bufs=2))
+        num_pool = ctx.enter_context(tc.psum_pool(name="nump", bufs=1))
+        rot_pool = ctx.enter_context(tc.psum_pool(name="rotp", bufs=3))
+        misc_pool = ctx.enter_context(tc.psum_pool(name="miscp", bufs=1))
+        ctx.enter_context(tc.manual_schedule())
+
+        ident = keep.tile([P, P], F32, name="ident")
+        one = keep.tile([P, 1], F32, name="one")
+        wk = keep.tile([P, A], U32, name="wk", align_bytes=64)
+        wv = keep.tile([P, A], U32, name="wv", align_bytes=64)
+        wq = keep.tile([P, A], U32, name="wq", align_bytes=64)
+        wo = keep.tile([P, A], U32, name="wo", align_bytes=64)
+        kpl = keep.tile([P, A], U8, name="kpl", align_bytes=64)
+        vpl = keep.tile([P, A], U8, name="vpl", align_bytes=64)
+        zby_a = keep.tile([P, 2, L], U8, name="zby_a", align_bytes=64)
+        zby_b = keep.tile([P, 6, L], U8, name="zby_b", align_bytes=64)
+        sc = keep.tile([P, 4], F32, name="sc")
+        zq_in = keep.tile([P, L], BF16, name="zq_in", align_bytes=64)
+        den = keep.tile([P, A], F32, name="den")
+        nm = keep.tile([P, W], F32, name="nm")
+        tq = keep.tile([P, A], F32, name="tq")
+        tT = [keep.tile([P, 512], F32, name="tT%d" % g) for g in range(G)]
+
+        nc.vector.memset(kpl[:].bitcast(U32), 0)
+        nc.vector.memset(one[:], 1.0)
+        nc.vector.memset(vpl[:].bitcast(U32), 0)
+        make_identity(nc, ident[:])
+
+        nc.sync.dma_start(out=zby_a[:], in_=z_window_bytes[0:2].rearrange("w b k -> b w k"))
+        nc.sync.dma_start(out=sc[:], in_=z_window_scale.rearrange("o c (p t) -> p (o c t)", t=4))
+
+        def load_scales(tile, k, src):
+            for q in range(4):
+                nc.sync.dma_start(out=tile[32 * q + k : 32 * q + k + 4, :].bitcast(I32), in_=src[4 * q : 4 * q + 4, :].bitcast(I32))
+
+        def load_words(tile, src, c0, c1):
+            nc.sync.dma_start(out=tile[:, c0:c1].bitcast(I32), in_=src.rearrange("p n t -> p (n t)")[:, 4 * c0 : 4 * c1].bitcast(I32))
+
+        load_scales(kpl, 0, Wk_scales[0])
+        load_words(wk, Wk_words[0], 0, 512)
+        load_words(wk, Wk_words[0], 512, 2048)
+        nc.sync.dma_start(out=zby_b[:], in_=z_window_bytes[2:8].rearrange("w b k -> b w k"))
+        nc.sync.dma_start(out=zq_in[:], in_=z_current)
+        load_scales(vpl, 4, Wq_scales[0])
+        load_scales(vpl, 0, Wv_scales[0])
+        for q in range(4):
+            nc.sync.dma_start(out=vpl[32 * q + 8 : 32 * q + 12, :].bitcast(I32).rearrange("p (g n) -> p g n", g=G), in_=Wo_scales.bitcast(I32)[:, 4 * q : 4 * q + 4, :].rearrange("g q n -> q g n"))
+        for h in range(2):
+            load_words(wq, Wq_words[0], 1024 * h, 1024 * h + 1024)
+        for h in range(2):
+            load_words(wv, Wv_words[0], 1024 * h, 1024 * h + 1024)
+        nc.sync.dma_start(out=wo[:].bitcast(I32).rearrange("p (g n) -> p g n", g=G), in_=Wo_words.rearrange("g p n t -> p g (n t)").bitcast(I32))
+
+        dummy = keep.tile([P, 1], F32, name="dummy")
+        nc.scalar.activation(out=dummy[:], in_=one[:], func=ACT.Exp)
+
+        zb = {}
+        zps = {}
+        zgr = {}
+        zcode = {}
+
+        def z_widen(ws, engine):
+            n = len(ws)
+            t = keep.tile([P, n, L], BF16, name="zb%d" % ws[0], align_bytes=64)
+            src = zby_a[:, ws[0] : ws[0] + n, :] if ws[0] < 2 else zby_b[:, ws[0] - 2 : ws[0] - 2 + n, :]
+            if engine == "v":
+                nc.vector.tensor_copy(out=t[:], in_=src.bitcast(FP8))
+            else:
+                nc.scalar.copy(out=t[:], in_=src.bitcast(FP8))
+            zb[ws[0]] = t
+
+        def z_turn(ws):
+            n = len(ws)
+            ps = misc_pool.tile([P, 512], F32, name="misc", tag="misc")
+            for i in range(n):
+                words = zb[ws[0]][:, i, :].bitcast(F32)
+                for u in range(2):
+                    nc.tensor.transpose(ps[:, u * 128 * n + i * 128 : u * 128 * n + i * 128 + 128], words[:, u : 256 : 2], ident[:])
+            zps[ws[0]] = ps
+
+        def z_scale(ws):
+            n = len(ws)
+            R = 128 * n
+            t = keep.tile([P, 4 * R], BF16, name="zgr%d" % ws[0], align_bytes=64)
+            nc.vector.tensor_tensor(
+                out=t[:].rearrange("p (r u e) -> p r u e", u=2, e=2),
+                in0=zps[ws[0]][:, : 2 * R].bitcast(BF16).rearrange("p (u r e) -> p r u e", u=2, e=2),
+                in1=sc[:].rearrange("p (u e) -> p u e", u=2).unsqueeze(1).to_broadcast([P, R, 2, 2]),
+                op=ALU.mult,
+            )
+            zgr[ws[0]] = t
+
+        def z_quant(ws):
+            n = len(ws)
+            R = 128 * n
+            c = keep.tile([P, R], U32, name="zc%d" % ws[0], align_bytes=64)
+            s = keep.tile([P, R], U8, name="zs%d" % ws[0], align_bytes=64)
+            nc.vector.quantize_mx(out=c[:].bitcast(FP8X4), scales=s[:], in_=zgr[ws[0]][:])
+            for i in range(n):
+                zcode[ws[0] + i] = (c[:, 128 * i : 128 * i + 128], s[:, 128 * i : 128 * i + 128])
+
+        def mm(ps, code, w_tile, plane, k, c0, n, start=True, stop=True):
+            nc.tensor.matmul_mx(
+                out=ps,
+                lhsT=code[0].bitcast(FP8X4),
+                lhsT_scale=code[1],
+                rhs=w_tile[:, c0 : c0 + n].bitcast(FP8X4),
+                rhs_scale=plane[k:P, c0 : c0 + n],
+                start=start,
+                stop=stop,
+            )
+
+        nk = {}
+        mn = {}
+        e = {}
+        ev = {}
+        rot = {}
+
+        def K_mm(w, g):
+            ps = rot_pool.tile([P, 512], F32, name="rot", tag="rot")
+            mm(ps[:], zcode[w], wk, kpl, 0, 512 * g, 512)
+            rot["k", w, g] = ps
+
+        def K_copy(w, g):
+            if g == 0:
+                nk[w] = keep.tile([P, A], F32, name="nk%d" % (w % 4), tag="nk%d" % (w % 4))
+                mn[w] = work.tile([P, G], F32, name="mn", tag="mn")
+            nc.vector.tensor_scalar(
+                out=nk[w][:, 512 * g : 512 * g + 512].rearrange("p (t m) -> p t m", t=4),
+                in0=rot["k", w, g][:].rearrange("p (m t) -> p t m", t=4),
+                scalar1=-1.0,
+                scalar2=None,
+                op0=ALU.mult,
+                op1=ALU.min,
+                accum_out=mn[w][:, g : g + 1],
+            )
+
+        def M_a(w):
+            m1 = work.tile([P, 1], F32, name="m1", tag="m1")
+            nc.vector.tensor_reduce(out=m1[:], in_=mn[w][:], axis=AX.X, op=ALU.min)
+            ps = misc_pool.tile([P, 512], F32, name="misc", tag="misc")
+            nc.tensor.transpose(ps[:, 0:128], m1[:].to_broadcast([P, P]), ident[:])
+            rot["m", w] = ps
+
+        def M_b(w):
+            nc.vector.tensor_reduce(out=nm[:, w : w + 1], in_=rot["m", w][:, 0:128], axis=AX.X, op=ALU.min)
+
+        def E(w, parts):
+            e[w] = keep.tile([P, A], F32, name="e%d" % w)
+            n = A // parts
+            for i in range(parts):
+                nc.scalar.activation(out=e[w][:, n * i : n * i + n], in_=nk[w][:, n * i : n * i + n], func=ACT.Exp, bias=nm[:, w : w + 1], scale=-1.0)
+
+        def D(w):
+            if w == 0 or w in PE_DEN:
+                return
+            for g in range(G):
+                c = slice(512 * g, 512 * g + 512)
+                nc.gpsimd.tensor_tensor(out=den[:, c], in0=e[0][:, c] if w == 1 else den[:, c], in1=e[w][:, c], op=ALU.add)
+
+        num = [None] * G
+
+        def P_mm(w, g):
+            ps = rot_pool.tile([P, 512], F32, name="rot", tag="rot")
+            mm(ps[:], zcode[w], wv, vpl, 0, 512 * g, 512)
+            rot["v", w, g] = ps
+
+        def P_v(w, g):
+            t = work.tile([P, 512], F32, name="ev%d" % g, tag="ev%d" % g)
+            nc.vector.tensor_tensor(
+                out=t[:].rearrange("p (t m) -> p t m", t=4),
+                in0=e[w][:, 512 * g : 512 * g + 512].rearrange("p (t m) -> p t m", t=4),
+                in1=rot["v", w, g][:].rearrange("p (m t) -> p t m", t=4),
+                op=ALU.mult,
+            )
+            ev[w, g] = t
+
+        def P_g(w, g):
+            v = work.tile([P, 512], F32, name="vs", tag="vs")
+            nc.scalar.copy(out=v[:].rearrange("p (t m) -> p t m", t=4), in_=rot["v", w, g][:].rearrange("p (m t) -> p t m", t=4))
+            t = work.tile([P, 512], F32, name="ev%d" % g, tag="ev%d" % g)
+            nc.gpsimd.tensor_tensor(out=t[:], in0=e[w][:, 512 * g : 512 * g + 512], in1=v[:], op=ALU.mult)
+            ev[w, g] = t
+
+        def T(w, g):
+            if w == 0:
+                num[g] = num_pool.tile([P, 512], F32, name="num%d" % g, tag="num%d" % g)
+            for t in range(4):
+                c = slice(128 * t, 128 * t + 128)
+                nc.tensor.matmul(num[g][:, c], lhsT=ev[w, g][:, c], rhs=ident[:], start=(w == 0 and t == 0), stop=(w == W - 1 and t == 3), is_transpose=True)
+
+        def q_turn():
+            ps = misc_pool.tile([P, 512], F32, name="misc", tag="misc")
+            words = zq_in[:].bitcast(F32)
+            for u in range(2):
+                nc.tensor.transpose(ps[:, u * 128 : u * 128 + 128], words[:, u : 256 : 2], ident[:])
+            t = keep.tile([P, 512], BF16, name="zqg", align_bytes=64)
+            nc.scalar.copy(out=t[:].bitcast(F32).rearrange("p (r u) -> p r u", u=2), in_=ps[:, 0:256].rearrange("p (u r) -> p r u", u=2))
+            zgr["q"] = t
+
+        def q_quant():
+            c = keep.tile([P, 128], U32, name="zcq", align_bytes=64)
+            s = keep.tile([P, 128], U8, name="zsq", align_bytes=64)
+            nc.vector.quantize_mx(out=c[:].bitcast(FP8X4), scales=s[:], in_=zgr["q"][:])
+            zcode["q"] = (c[:], s[:])
+
+        def q_mm(g):
+            ps = num_pool.tile([P, 512], F32, name="num%d" % g, tag="num%d" % g)
+            mm(ps[:], zcode["q"], wq, vpl, 4, 512 * g, 512)
+            nc.scalar.activation(out=tq[:, 512 * g : 512 * g + 512].rearrange("p (t m) -> p t m", t=4), in_=ps[:].rearrange("p (m t) -> p t m", t=4), func=ACT.Tanh, scale=0.5)
+
+        def q_T(g):
+            ps = num_pool.tile([P, 512], F32, name="num%d" % g, tag="num%d" % g)
+            for t in range(4):
+                c = slice(128 * t, 128 * t + 128)
+                nc.tensor.transpose(ps[:, c], tq[:, 512 * g + 128 * t : 512 * g + 128 * t + 128], ident[:])
+            nc.scalar.activation(out=tT[g][:].rearrange("p (b t) -> p b t", t=4), in_=ps[:].rearrange("p (t b) -> p b t", t=4), func=ACT.Copy, bias=1.0)
+
+        ep = {}
+
+        def D_T(g):
+            if g % 2:
+                ps = rot_pool.tile([P, 512], F32, name="rot", tag="rot")
+            else:
+                ps = misc_pool.tile([P, 512], F32, name="misc", tag="misc")
+            srcs = [den] + [e[w] for w in PE_DEN]
+            for i in range(len(srcs)):
+                for t in range(4):
+                    c0 = 512 * g + 128 * t
+                    nc.tensor.matmul(ps[:, 128 * t : 128 * t + 128], lhsT=srcs[i][:, c0 : c0 + 128], rhs=ident[:], start=(i == 0 and t == 0), stop=(i == len(srcs) - 1 and t == 3), is_transpose=True)
+            s = work.tile([P, 512], F32, name="rs", tag="rs")
+            nc.scalar.activation(out=s[:].rearrange("p (b t) -> p b t", t=4), in_=ps[:].rearrange("p (t b) -> p b t", t=4), func=ACT.Abs_reciprocal_sqrt, bias=2.0 * EPS, scale=2.0)
+            r = work.tile([P, 512], F32, name="rr", tag="rr")
+            nc.scalar.activation(out=r[:], in_=s[:], func=ACT.Square)
+            ep["r", g] = r
+            c = keep.tile([P, 512], F32, name="cc%d" % g)
+            nc.gpsimd.tensor_tensor(out=c[:], in0=tT[g][:], in1=r[:], op=ALU.mult)
+            ep["m", g] = c
+
+        def h_v(g):
+            t = work.tile([P, 512], BF16, name="hh", tag="hh", align_bytes=64)
+            nc.vector.tensor_tensor(
+                out=t[:].rearrange("p (b t) -> p b t", t=4),
+                in0=ep["m", g][:].rearrange("p (b t) -> p b t", t=4),
+                in1=num[g][:].rearrange("p (t b) -> p b t", t=4),
+                op=ALU.mult,
+            )
+            ep["h", g] = t
+
+        def h_q(g):
+            c = work.tile([P, 128], U32, name="hc", tag="hc", align_bytes=64)
+            s = work.tile([P, 128], U8, name="hs", tag="hs", align_bytes=64)
+            nc.vector.quantize_mx(out=c[:].bitcast(FP8X4), scales=s[:], in_=ep["h", g][:])
+            ep["c", g] = (c[:], s[:])
+
+        def o_mm(g):
+            for i in range(2):
+                if g == 0:
+                    ep["o", i] = num_pool.tile([P, 512], F32, name="num%d" % i, tag="num%d" % i)
+                mm(ep["o", i][:, 0:256], ep["c", g], wo, vpl, 8, 512 * g + 256 * i, 256, start=(g == 0), stop=(g == G - 1))
+
+        LAG = 3
+        GSET = {}
+        z_widen([0], "v")
+        z_turn([0])
+        z_widen([1], "s")
+        z_scale([0])
+        z_quant([0])
+        z_turn([1])
+        z_widen([2, 3], "s")
+        z_scale([1])
+        z_quant([1])
+
+        steps = []
+        for s in range(W + LAG):
+            pw = s - LAG
+            ks = [("k", s, g) for g in range(G)] if s < W else []
+            ps = [("g" if (pw, g) in GSET else "p", pw, g) for g in range(G)] if pw >= 0 else []
+            gs = [u for u in ps if u[0] == "g"]
+            ps = [u for u in ps if u[0] == "p"]
+            units = list(gs)
+            if s == W - 1:
+                units += ks + ps
+            else:
+                for g in range(G):
+                    units += ks[g : g + 1] + ps[g : g + 1]
+            steps.append(units)
+        flat = [u for st in steps for u in st]
+
+        def fill(i):
+            if i < len(flat):
+                kind, w, g = flat[i]
+                if kind == "k":
+                    K_mm(w, g)
+                else:
+                    P_mm(w, g)
+
+        turns = []
+
+        def T_flush(n):
+            for i in range(min(n, len(turns))):
+                T(*turns.pop(0))
+
+        for i in range(LOOK):
+            fill(i)
+        pos = 0
+        for s in range(W + LAG):
+            st = steps[s]
+            for j in range(len(st)):
+                fill(pos + LOOK)
+                pos += 1
+                kind, w, g = st[j]
+                if kind == "k":
+                    K_copy(w, g)
+                elif kind == "p":
+                    P_v(w, g)
+                else:
+                    P_g(w, g)
+                key = kind + str(g)
+                jj = j - len([u for u in st if u[0] == "g"])
+                if jj == 0 and 1 <= s < W:
+                    M_a(s - 1)
+                if jj == 1 and 1 <= s < W:
+                    M_b(s - 1)
+                    E(s - 1, 2)
+                    D(s - 1)
+                if s == W - 1 and jj == 4:
+                    M_a(s)
+                if s == W - 1 and jj == 5:
+                    M_b(s)
+                    E(s, 4)
+                    D(s)
+                    nc.scalar.activation(out=dummy[:], in_=one[:], func=ACT.Abs_reciprocal_sqrt)
+                for zs, zw in ((0, 2), (1, 4), (2, 6)):
+                    if s == zs:
+                        if key == "k1":
+                            if zw < 6:
+                                z_widen([zw + 2, zw + 3], "s")
+                            z_turn([zw, zw + 1])
+                        if key == "k2":
+                            z_scale([zw, zw + 1])
+                        if key == "k3":
+                            z_quant([zw, zw + 1])
+                if s == 0 and key == "k2":
+                    q_turn()
+                if s == 1 and key == "k0":
+                    q_quant()
+                if s == 2:
+                    if key == "k1":
+                        q_mm(0)
+                    if key == "k2":
+                        q_mm(1)
+                        q_mm(2)
+                    if key == "k3":
+                        q_mm(3)
+                        q_T(0)
+                if s == 3:
+                    if jj == 1:
+                        q_T(1)
+                        q_T(2)
+                        q_T(3)
+                if kind != "k":
+                    if not (pos >= len(flat) - 3):
+                        turns.append((w, g))
+                if len(turns) > 2 and s < W + LAG - 1:
+                    T_flush(2)
+                if s == W + LAG - 2 and key == "p3":
+                    D_T(0)
+                if s == W + LAG - 1:
+                    if key == "p0":
+                        T_flush(9)
+                        D_T(1)
+                        T(7, 0)
+                        D_T(2)
+                    if key == "p1":
+                        T(7, 1)
+                        D_T(3)
+                    if key == "p2":
+                        h_v(0)
+                        T(7, 2)
+                    if key == "p3":
+                        h_q(0)
+                        h_v(1)
+                        T(7, 3)
+                        h_q(1)
+                        h_v(2)
+                        o_mm(0)
+                        o_mm(1)
+                        h_q(2)
+                        h_v(3)
+                        h_q(3)
+                        o_mm(2)
+                        o_mm(3)
+        o_sb = keep.tile([P, 256], F32, name="o_sb")
+        o_sb2 = keep.tile([P, 256], F32, name="o_sb2")
+        nc.vector.tensor_copy(out=o_sb[:], in_=ep["o", 0][:, 0:256])
+        nc.sync.dma_start(out=out[:, 0:256], in_=o_sb[:])
+        nc.scalar.copy(out=o_sb2[:], in_=ep["o", 1][:, 0:256])
+        nc.sync.dma_start(out=out[:, 256:512], in_=o_sb2[:])

@@ -19,16 +19,319 @@ B, L, A, W = 128, 512, 2048, 8
 G = A // 512
 EPS = 1e-8
 FLOPS = 2 * B * L * A * (1 + 2 * W) + 2 * B * A * L
-PE_DEN = (7,)
-G_UNITS = ()
 LOOK = 2
+PARAM = {
+    "zv": [1],
+    "pe_den": [6,7],
+    "zw0": 0,
+    "zt0": 1,
+    "zw1": 3,
+    "zs0": 2,
+    "spt": 4,
+    "spc": 9,
+    "zq0": 5,
+    "zw2": 6,
+    "zm2": 15,
+    "fill0": 7,
+    "fill1": 16,
+    "fill2": 11,
+    "use0": 8,
+    "zt1": 13,
+    "zc1": 19,
+    "zw4": 14,
+    "zm4": 26,
+    "fill3": 10,
+    "use1": 20,
+    "zq1": 22,
+    "fill4": 25,
+    "use2": 17,
+    "fill5": 28,
+    "use3": 12,
+    "zt2": 30,
+    "zc2": 33,
+    "zw6": 18,
+    "zm6": 38,
+    "fill6": 29,
+    "use4": 27,
+    "mv0": 24,
+    "mp0": 35,
+    "fill7": 32,
+    "use5": 31,
+    "zq2": 36,
+    "mb0": 37,
+    "e0_0": 50,
+    "e0_1": 41,
+    "fill8": 52,
+    "use6": 34,
+    "fill9": 53,
+    "use7": 40,
+    "fill10": 39,
+    "use8": 57,
+    "mv1": 47,
+    "mp1": 55,
+    "fill11": 42,
+    "use9": 59,
+    "mb1": 62,
+    "e1_0": 73,
+    "e1_1": 65,
+    "d1": 76,
+    "fill12": 45,
+    "use10": 44,
+    "zt4": 43,
+    "zc4": 46,
+    "fill13": 49,
+    "use11": 48,
+    "ztq": 21,
+    "zcq": 23,
+    "fill14": 74,
+    "use12": 51,
+    "t0_0": 60,
+    "fill15": 79,
+    "use13": 54,
+    "zq4": 66,
+    "zqq": 63,
+    "u0_0": 58,
+    "u0_1": 56,
+    "t0_1": 67,
+    "fill16": 61,
+    "use14": 82,
+    "mv2": 68,
+    "mp2": 70,
+    "fill17": 64,
+    "use15": 84,
+    "mb2": 72,
+    "e2_0": 80,
+    "e2_1": 89,
+    "d2": 96,
+    "fill18": 71,
+    "use16": 69,
+    "zt6": 77,
+    "zc6": 85,
+    "fill19": 81,
+    "use17": 75,
+    "fill20": 99,
+    "use18": 78,
+    "t1_0": 86,
+    "fill21": 88,
+    "use19": 87,
+    "zq6": 91,
+    "u1_0": 92,
+    "u1_1": 83,
+    "t1_1": 95,
+    "fill22": 90,
+    "use20": 102,
+    "mv3": 93,
+    "mp3": 97,
+    "fill23": 103,
+    "use21": 94,
+    "mb3": 101,
+    "e3_0": 106,
+    "e3_1": 111,
+    "d3": 118,
+    "fill24": 100,
+    "use22": 98,
+    "fill25": 109,
+    "use23": 108,
+    "qt0": 107,
+    "fill26": 110,
+    "qo0": 117,
+    "use24": 104,
+    "fill27": 113,
+    "use25": 112,
+    "t2_0": 105,
+    "fill28": 116,
+    "use26": 115,
+    "u2_0": 123,
+    "u2_1": 119,
+    "t2_1": 114,
+    "fill29": 125,
+    "use27": 122,
+    "mv4": 120,
+    "mp4": 124,
+    "fill30": 127,
+    "use28": 121,
+    "mb4": 126,
+    "e4_0": 128,
+    "e4_1": 134,
+    "d4": 141,
+    "fill31": 130,
+    "use29": 129,
+    "fill32": 133,
+    "use30": 132,
+    "qt1": 131,
+    "fill33": 136,
+    "qo1": 140,
+    "use31": 135,
+    "fill34": 139,
+    "use32": 138,
+    "t3_0": 137,
+    "fill35": 145,
+    "use33": 143,
+    "u3_0": 150,
+    "u3_1": 142,
+    "t3_1": 153,
+    "fill36": 146,
+    "use34": 144,
+    "mv5": 147,
+    "mp5": 152,
+    "fill37": 149,
+    "use35": 148,
+    "mb5": 154,
+    "e5_0": 157,
+    "e5_1": 162,
+    "d5": 169,
+    "fill38": 156,
+    "use36": 151,
+    "fill39": 158,
+    "use37": 155,
+    "qt2": 160,
+    "fill40": 161,
+    "qo2": 168,
+    "use38": 159,
+    "fill41": 172,
+    "use39": 163,
+    "t4_0": 167,
+    "fill42": 176,
+    "use40": 166,
+    "u4_0": 165,
+    "u4_1": 171,
+    "t4_1": 178,
+    "fill43": 164,
+    "use41": 175,
+    "mv6": 173,
+    "mp6": 179,
+    "fill44": 174,
+    "use42": 180,
+    "mb6": 183,
+    "e6_0": 191,
+    "e6_1": 185,
+    "fill45": 182,
+    "use43": 170,
+    "fill46": 184,
+    "use44": 177,
+    "qt3": 188,
+    "fill47": 187,
+    "qo3": 197,
+    "use45": 186,
+    "fill48": 192,
+    "use46": 189,
+    "t5_0": 190,
+    "fill49": 194,
+    "use47": 193,
+    "u5_0": 181,
+    "u5_1": 195,
+    "t5_1": 199,
+    "fill50": 200,
+    "use48": 201,
+    "mv7": 196,
+    "mp7": 202,
+    "u6_0": 203,
+    "u6_1": 205,
+    "fill51": 208,
+    "use49": 198,
+    "mb7": 204,
+    "e7_0": 212,
+    "e7_1": 207,
+    "tab": 218,
+    "fill52": 215,
+    "use50": 206,
+    "fill53": 217,
+    "use51": 210,
+    "fill54": 209,
+    "use52": 220,
+    "u7_0": 221,
+    "u7_1": 223,
+    "t6_0": 213,
+    "fill55": 211,
+    "use53": 222,
+    "t6_1": 219,
+    "t7_0": 225,
+    "t7_1": 226,
+    "fill56": 228,
+    "n2_0": 227,
+    "ro0": 224,
+    "sq0": 237,
+    "n2_1": 229,
+    "ro1": 234,
+    "sq1": 240,
+    "t0_2": 231,
+    "t0_3": 233,
+    "use54": 214,
+    "t1_2": 235,
+    "fill57": 230,
+    "use55": 216,
+    "t1_3": 239,
+    "fill58": 242,
+    "h0": 241,
+    "h1": 244,
+    "use56": 232,
+    "t2_2": 238,
+    "fill59": 243,
+    "hq0": 255,
+    "hq1": 249,
+    "use57": 236,
+    "t2_3": 246,
+    "fill60": 245,
+    "use58": 247,
+    "t3_2": 252,
+    "fill61": 256,
+    "use59": 250,
+    "t3_3": 254,
+    "fill62": 258,
+    "use60": 251,
+    "dt2": 248,
+    "ro2": 253,
+    "sq2": 257,
+    "t4_2": 261,
+    "fill63": 260,
+    "use61": 262,
+    "t4_3": 265,
+    "fill64": 267,
+    "use62": 259,
+    "t5_2": 271,
+    "fill65": 274,
+    "use63": 264,
+    "t5_3": 273,
+    "fill66": 268,
+    "use64": 269,
+    "dt3": 263,
+    "ro3": 266,
+    "sq3": 270,
+    "t6_2": 277,
+    "fill67": 275,
+    "use65": 276,
+    "t6_3": 280,
+    "use66": 272,
+    "t7_2": 279,
+    "use67": 278,
+    "om0_0": 283,
+    "om0_1": 285,
+    "t7_3": 282,
+    "om1_0": 286,
+    "om1_1": 287,
+    "n2_2": 281,
+    "n2_3": 284,
+    "h2": 288,
+    "hq2": 290,
+    "h3": 289,
+    "om2_0": 292,
+    "om2_1": 294,
+    "hq3": 291,
+    "om3_0": 293,
+    "om3_1": 295,
+    "oo0": 296,
+    "oo1": 297,
+}
 
 
 def tile_aftblock_pa_w8_kernel(tc, z_current, z_window_bytes, z_window_scale, Wq_words, Wq_scales, Wk_words, Wk_scales, Wv_words, Wv_scales, Wo_words, Wo_scales, out):
     nc = tc.nc
+    PE_DEN = PARAM.get("pe_den", (7,))
+    ZV = PARAM.get("zv", ())
     with ExitStack() as ctx:
         keep = ctx.enter_context(tc.tile_pool(name="keep", bufs=1))
         work = ctx.enter_context(tc.tile_pool(name="work", bufs=2))
+        ev_pool = ctx.enter_context(tc.tile_pool(name="evp", bufs=4))
         num_pool = ctx.enter_context(tc.psum_pool(name="nump", bufs=1))
         rot_pool = ctx.enter_context(tc.psum_pool(name="rotp", bufs=3))
         misc_pool = ctx.enter_context(tc.psum_pool(name="miscp", bufs=1))
@@ -42,11 +345,11 @@ def tile_aftblock_pa_w8_kernel(tc, z_current, z_window_bytes, z_window_scale, Wq
         wo = keep.tile([P, A], U32, name="wo", align_bytes=64)
         kpl = keep.tile([P, A], U8, name="kpl", align_bytes=64)
         vpl = keep.tile([P, A], U8, name="vpl", align_bytes=64)
-        zby_a = keep.tile([P, 2, L], U8, name="zby_a", align_bytes=64)
-        zby_b = keep.tile([P, 6, L], U8, name="zby_b", align_bytes=64)
+        ZCUT = (0, 1, 4, 8)
+        zby = [keep.tile([P, ZCUT[i + 1] - ZCUT[i], L], U8, name="zby%d" % i, align_bytes=64) for i in range(3)]
         sc = keep.tile([P, 4], F32, name="sc")
         zq_in = keep.tile([P, L], BF16, name="zq_in", align_bytes=64)
-        den = keep.tile([P, A], F32, name="den")
+        den = keep.tile([P, 1024], F32, name="den")
         nm = keep.tile([P, W], F32, name="nm")
         tq = keep.tile([P, A], F32, name="tq")
         tT = [keep.tile([P, 512], F32, name="tT%d" % g) for g in range(G)]
@@ -54,10 +357,13 @@ def tile_aftblock_pa_w8_kernel(tc, z_current, z_window_bytes, z_window_scale, Wq
         nc.vector.memset(kpl[:].bitcast(U32), 0)
         nc.vector.memset(one[:], 1.0)
         nc.vector.memset(vpl[:].bitcast(U32), 0)
+        nc.gpsimd.dma_start(out=sc[:], in_=z_window_scale.rearrange("o c (p t) -> p (o c t)", t=4))
         make_identity(nc, ident[:])
 
-        nc.sync.dma_start(out=zby_a[:], in_=z_window_bytes[0:2].rearrange("w b k -> b w k"))
-        nc.sync.dma_start(out=sc[:], in_=z_window_scale.rearrange("o c (p t) -> p (o c t)", t=4))
+        def load_z(i):
+            nc.sync.dma_start(out=zby[i][:], in_=z_window_bytes[ZCUT[i] : ZCUT[i + 1]].rearrange("w b k -> b w k"))
+
+        load_z(0)
 
         def load_scales(tile, k, src):
             for q in range(4):
@@ -68,66 +374,21 @@ def tile_aftblock_pa_w8_kernel(tc, z_current, z_window_bytes, z_window_scale, Wq
 
         load_scales(kpl, 0, Wk_scales[0])
         load_words(wk, Wk_words[0], 0, 512)
+        load_z(1)
         load_words(wk, Wk_words[0], 512, 2048)
-        nc.sync.dma_start(out=zby_b[:], in_=z_window_bytes[2:8].rearrange("w b k -> b w k"))
+        load_z(2)
         nc.sync.dma_start(out=zq_in[:], in_=z_current)
-        load_scales(vpl, 4, Wq_scales[0])
         load_scales(vpl, 0, Wv_scales[0])
+        load_scales(vpl, 4, Wq_scales[0])
         for q in range(4):
             nc.sync.dma_start(out=vpl[32 * q + 8 : 32 * q + 12, :].bitcast(I32).rearrange("p (g n) -> p g n", g=G), in_=Wo_scales.bitcast(I32)[:, 4 * q : 4 * q + 4, :].rearrange("g q n -> q g n"))
-        for h in range(2):
-            load_words(wq, Wq_words[0], 1024 * h, 1024 * h + 1024)
-        for h in range(2):
-            load_words(wv, Wv_words[0], 1024 * h, 1024 * h + 1024)
+        for tl, src in ((wv, Wv_words), (wq, Wq_words)):
+            for h in range(2):
+                load_words(tl, src[0], 1024 * h, 1024 * h + 1024)
         nc.sync.dma_start(out=wo[:].bitcast(I32).rearrange("p (g n) -> p g n", g=G), in_=Wo_words.rearrange("g p n t -> p g (n t)").bitcast(I32))
 
         dummy = keep.tile([P, 1], F32, name="dummy")
         nc.scalar.activation(out=dummy[:], in_=one[:], func=ACT.Exp)
-
-        zb = {}
-        zps = {}
-        zgr = {}
-        zcode = {}
-
-        def z_widen(ws, engine):
-            n = len(ws)
-            t = keep.tile([P, n, L], BF16, name="zb%d" % ws[0], align_bytes=64)
-            src = zby_a[:, ws[0] : ws[0] + n, :] if ws[0] < 2 else zby_b[:, ws[0] - 2 : ws[0] - 2 + n, :]
-            if engine == "v":
-                nc.vector.tensor_copy(out=t[:], in_=src.bitcast(FP8))
-            else:
-                nc.scalar.copy(out=t[:], in_=src.bitcast(FP8))
-            zb[ws[0]] = t
-
-        def z_turn(ws):
-            n = len(ws)
-            ps = misc_pool.tile([P, 512], F32, name="misc", tag="misc")
-            for i in range(n):
-                words = zb[ws[0]][:, i, :].bitcast(F32)
-                for u in range(2):
-                    nc.tensor.transpose(ps[:, u * 128 * n + i * 128 : u * 128 * n + i * 128 + 128], words[:, u : 256 : 2], ident[:])
-            zps[ws[0]] = ps
-
-        def z_scale(ws):
-            n = len(ws)
-            R = 128 * n
-            t = keep.tile([P, 4 * R], BF16, name="zgr%d" % ws[0], align_bytes=64)
-            nc.vector.tensor_tensor(
-                out=t[:].rearrange("p (r u e) -> p r u e", u=2, e=2),
-                in0=zps[ws[0]][:, : 2 * R].bitcast(BF16).rearrange("p (u r e) -> p r u e", u=2, e=2),
-                in1=sc[:].rearrange("p (u e) -> p u e", u=2).unsqueeze(1).to_broadcast([P, R, 2, 2]),
-                op=ALU.mult,
-            )
-            zgr[ws[0]] = t
-
-        def z_quant(ws):
-            n = len(ws)
-            R = 128 * n
-            c = keep.tile([P, R], U32, name="zc%d" % ws[0], align_bytes=64)
-            s = keep.tile([P, R], U8, name="zs%d" % ws[0], align_bytes=64)
-            nc.vector.quantize_mx(out=c[:].bitcast(FP8X4), scales=s[:], in_=zgr[ws[0]][:])
-            for i in range(n):
-                zcode[ws[0] + i] = (c[:, 128 * i : 128 * i + 128], s[:, 128 * i : 128 * i + 128])
 
         def mm(ps, code, w_tile, plane, k, c0, n, start=True, stop=True):
             nc.tensor.matmul_mx(
@@ -140,290 +401,329 @@ def tile_aftblock_pa_w8_kernel(tc, z_current, z_window_bytes, z_window_scale, Wq
                 stop=stop,
             )
 
-        nk = {}
-        mn = {}
-        e = {}
-        ev = {}
-        rot = {}
+        def tm(ap):
+            return ap.rearrange("p (t m) -> p t m", t=4)
+
+        def mt(ap):
+            return ap.rearrange("p (m t) -> p t m", t=4)
+
+        def bt(ap):
+            return ap.rearrange("p (b t) -> p b t", t=4)
+
+        def tb(ap):
+            return ap.rearrange("p (t b) -> p b t", t=4)
+
+        X = {}
+
+        def rot_tile():
+            return rot_pool.tile([P, 512], F32, name="rot", tag="rot")
+
+        def misc_tile():
+            return misc_pool.tile([P, 512], F32, name="misc", tag="misc")
+
+        scb = keep.tile([P, L], F32, name="scb")
+
+        def z_widen(w, n, vec=False):
+            t = keep.tile([P, n, L], BF16, name="zb%d" % w, align_bytes=64)
+            i = max(i for i in range(3) if ZCUT[i] <= w)
+            src = zby[i][:, w - ZCUT[i] : w - ZCUT[i] + n, :].bitcast(FP8)
+            if vec:
+                nc.vector.tensor_copy(out=t[:], in_=src)
+            else:
+                nc.scalar.copy(out=t[:], in_=src)
+            X["zb", w] = t
+            if vec or w in ZV:
+                X["zt", w] = t
+
+        def z_mul(w, n):
+            t = keep.tile([P, n, L], BF16, name="zm%d" % w, align_bytes=64)
+            nc.gpsimd.tensor_tensor(out=t[:], in0=X["zb", w][:], in1=scb[:].unsqueeze(1).to_broadcast([P, n, L]), op=ALU.mult)
+            X["zt", w] = t
+
+        def z_turn(w, n):
+            ps = misc_tile()
+            for i in range(n):
+                words = X["zt", w][:, i, :].bitcast(F32)
+                for u in range(2):
+                    nc.tensor.transpose(ps[:, u * 128 * n + i * 128 : u * 128 * n + i * 128 + 128], words[:, u : 256 : 2], ident[:])
+            X["zp", w] = ps
+
+        def z_scale(w, n):
+            R = 128 * n
+            t = keep.tile([P, 4 * R], BF16, name="zgr%d" % w, align_bytes=64)
+            nc.vector.tensor_tensor(
+                out=t[:].rearrange("p (r u e) -> p r u e", u=2, e=2),
+                in0=X["zp", w][:, : 2 * R].bitcast(BF16).rearrange("p (u r e) -> p r u e", u=2, e=2),
+                in1=sc[:].rearrange("p (u e) -> p u e", u=2).unsqueeze(1).to_broadcast([P, R, 2, 2]),
+                op=ALU.mult,
+            )
+            X["zg", w] = t
+
+        def z_copy(w, n):
+            t = keep.tile([P, 512 * n], BF16, name="zgr%s" % w, align_bytes=64)
+            nc.scalar.copy(out=t[:].bitcast(F32).rearrange("p (r u) -> p r u", u=2), in_=X["zp", w][:, : 256 * n].rearrange("p (u r) -> p r u", u=2))
+            X["zg", w] = t
+
+        def z_quant(w, n):
+            c = keep.tile([P, 128 * n], U32, name="zc%s" % w, align_bytes=64)
+            s = keep.tile([P, 128 * n], U8, name="zs%s" % w, align_bytes=64)
+            nc.vector.quantize_mx(out=c[:].bitcast(FP8X4), scales=s[:], in_=X["zg", w][:])
+            for i in range(n):
+                X["z", w if w == "q" else w + i] = (c[:, 128 * i : 128 * i + 128], s[:, 128 * i : 128 * i + 128])
+
+        def spread_turn():
+            ps = misc_tile()
+            for t in range(4):
+                nc.tensor.transpose(ps[:, 128 * t : 128 * t + 128], sc[:, t : t + 1].to_broadcast([P, P]), ident[:])
+            X["sp"] = ps
+
+        def spread_copy():
+            nc.scalar.copy(out=scb[:].rearrange("p (m t) -> p m t", t=4), in_=X["sp"][:].rearrange("p (t m) -> p m t", t=4))
 
         def K_mm(w, g):
-            ps = rot_pool.tile([P, 512], F32, name="rot", tag="rot")
-            mm(ps[:], zcode[w], wk, kpl, 0, 512 * g, 512)
-            rot["k", w, g] = ps
+            ps = rot_tile()
+            mm(ps[:], X["z", w], wk, kpl, 0, 512 * g, 512)
+            X["k", w, g] = ps
 
         def K_copy(w, g):
-            if g == 0:
-                nk[w] = keep.tile([P, A], F32, name="nk%d" % (w % 4), tag="nk%d" % (w % 4))
-                mn[w] = work.tile([P, G], F32, name="mn", tag="mn")
+            if ("nk", w) not in X:
+                X["nk", w] = keep.tile([P, A], F32, name="nk%d" % (w % 4), tag="nk%d" % (w % 4))
+                X["mn", w] = work.tile([P, G], F32, name="mn", tag="mn")
             nc.vector.tensor_scalar(
-                out=nk[w][:, 512 * g : 512 * g + 512].rearrange("p (t m) -> p t m", t=4),
-                in0=rot["k", w, g][:].rearrange("p (m t) -> p t m", t=4),
+                out=tm(X["nk", w][:, 512 * g : 512 * g + 512]),
+                in0=mt(X["k", w, g][:]),
                 scalar1=-1.0,
                 scalar2=None,
                 op0=ALU.mult,
                 op1=ALU.min,
-                accum_out=mn[w][:, g : g + 1],
+                accum_out=X["mn", w][:, g : g + 1],
             )
 
-        def M_a(w):
+        def M_v(w):
             m1 = work.tile([P, 1], F32, name="m1", tag="m1")
-            nc.vector.tensor_reduce(out=m1[:], in_=mn[w][:], axis=AX.X, op=ALU.min)
-            ps = misc_pool.tile([P, 512], F32, name="misc", tag="misc")
-            nc.tensor.transpose(ps[:, 0:128], m1[:].to_broadcast([P, P]), ident[:])
-            rot["m", w] = ps
+            nc.vector.tensor_reduce(out=m1[:], in_=X["mn", w][:], axis=AX.X, op=ALU.min)
+            X["m1", w] = m1
+
+        def M_pe(w):
+            ps = misc_tile()
+            nc.tensor.transpose(ps[:, 0:128], X["m1", w][:].to_broadcast([P, P]), ident[:])
+            X["m", w] = ps
 
         def M_b(w):
-            nc.vector.tensor_reduce(out=nm[:, w : w + 1], in_=rot["m", w][:, 0:128], axis=AX.X, op=ALU.min)
+            nc.vector.tensor_reduce(out=nm[:, w : w + 1], in_=X["m", w][:, 0:128], axis=AX.X, op=ALU.min)
 
-        def E(w, parts):
-            e[w] = keep.tile([P, A], F32, name="e%d" % w)
+        def E(w, i, parts):
+            if ("e", w) not in X:
+                X["e", w] = keep.tile([P, A], F32, name="e%d" % w)
             n = A // parts
-            for i in range(parts):
-                nc.scalar.activation(out=e[w][:, n * i : n * i + n], in_=nk[w][:, n * i : n * i + n], func=ACT.Exp, bias=nm[:, w : w + 1], scale=-1.0)
+            nc.scalar.activation(out=X["e", w][:, n * i : n * i + n], in_=X["nk", w][:, n * i : n * i + n], func=ACT.Exp, bias=nm[:, w : w + 1], scale=-1.0)
 
         def D(w):
-            if w == 0 or w in PE_DEN:
-                return
-            for g in range(G):
-                c = slice(512 * g, 512 * g + 512)
-                nc.gpsimd.tensor_tensor(out=den[:, c], in0=e[0][:, c] if w == 1 else den[:, c], in1=e[w][:, c], op=ALU.add)
+            nc.gpsimd.tensor_tensor(out=den[:], in0=X["e", 0][:, 1024:] if w == 1 else den[:], in1=X["e", w][:, 1024:], op=ALU.add)
 
         num = [None] * G
 
         def P_mm(w, g):
-            ps = rot_pool.tile([P, 512], F32, name="rot", tag="rot")
-            mm(ps[:], zcode[w], wv, vpl, 0, 512 * g, 512)
-            rot["v", w, g] = ps
+            ps = rot_tile()
+            mm(ps[:], X["z", w], wv, vpl, 0, 512 * g, 512)
+            X["v", w, g] = ps
 
         def P_v(w, g):
-            t = work.tile([P, 512], F32, name="ev%d" % g, tag="ev%d" % g)
-            nc.vector.tensor_tensor(
-                out=t[:].rearrange("p (t m) -> p t m", t=4),
-                in0=e[w][:, 512 * g : 512 * g + 512].rearrange("p (t m) -> p t m", t=4),
-                in1=rot["v", w, g][:].rearrange("p (m t) -> p t m", t=4),
-                op=ALU.mult,
-            )
-            ev[w, g] = t
+            t = ev_pool.tile([P, 512], F32, name="ev%d" % (g % 2), tag="ev%d" % (g % 2))
+            nc.vector.tensor_tensor(out=tm(t[:]), in0=tm(X["e", w][:, 512 * g : 512 * g + 512]), in1=mt(X["v", w, g][:]), op=ALU.mult)
+            X["ev", w, g] = t
+
+        def P_s(w, g):
+            v = work.tile([P, 512], F32, name="vs", tag="vs")
+            nc.scalar.copy(out=tm(v[:]), in_=mt(X["v", w, g][:]))
+            X["vs", w, g] = v
 
         def P_g(w, g):
-            v = work.tile([P, 512], F32, name="vs", tag="vs")
-            nc.scalar.copy(out=v[:].rearrange("p (t m) -> p t m", t=4), in_=rot["v", w, g][:].rearrange("p (m t) -> p t m", t=4))
-            t = work.tile([P, 512], F32, name="ev%d" % g, tag="ev%d" % g)
-            nc.gpsimd.tensor_tensor(out=t[:], in0=e[w][:, 512 * g : 512 * g + 512], in1=v[:], op=ALU.mult)
-            ev[w, g] = t
+            t = ev_pool.tile([P, 512], F32, name="ev%d" % (g % 2), tag="ev%d" % (g % 2))
+            nc.gpsimd.tensor_tensor(out=t[:], in0=X["e", w][:, 512 * g : 512 * g + 512], in1=X["vs", w, g][:], op=ALU.mult)
+            X["ev", w, g] = t
 
         def T(w, g):
             if w == 0:
-                num[g] = num_pool.tile([P, 512], F32, name="num%d" % g, tag="num%d" % g)
+                num[g] = num_pool.tile([P, 512], F32, name="n%d" % (g % 2), tag="n%d" % (g % 2))
             for t in range(4):
                 c = slice(128 * t, 128 * t + 128)
-                nc.tensor.matmul(num[g][:, c], lhsT=ev[w, g][:, c], rhs=ident[:], start=(w == 0 and t == 0), stop=(w == W - 1 and t == 3), is_transpose=True)
+                nc.tensor.matmul(num[g][:, c], lhsT=X["ev", w, g][:, c], rhs=ident[:], start=(w == 0 and t == 0), stop=(w == W - 1 and t == 3), is_transpose=True)
 
         def q_turn():
-            ps = misc_pool.tile([P, 512], F32, name="misc", tag="misc")
+            ps = misc_tile()
             words = zq_in[:].bitcast(F32)
             for u in range(2):
                 nc.tensor.transpose(ps[:, u * 128 : u * 128 + 128], words[:, u : 256 : 2], ident[:])
-            t = keep.tile([P, 512], BF16, name="zqg", align_bytes=64)
-            nc.scalar.copy(out=t[:].bitcast(F32).rearrange("p (r u) -> p r u", u=2), in_=ps[:, 0:256].rearrange("p (u r) -> p r u", u=2))
-            zgr["q"] = t
-
-        def q_quant():
-            c = keep.tile([P, 128], U32, name="zcq", align_bytes=64)
-            s = keep.tile([P, 128], U8, name="zsq", align_bytes=64)
-            nc.vector.quantize_mx(out=c[:].bitcast(FP8X4), scales=s[:], in_=zgr["q"][:])
-            zcode["q"] = (c[:], s[:])
+            X["zp", "q"] = ps
 
         def q_mm(g):
-            ps = num_pool.tile([P, 512], F32, name="num%d" % g, tag="num%d" % g)
-            mm(ps[:], zcode["q"], wq, vpl, 4, 512 * g, 512)
-            nc.scalar.activation(out=tq[:, 512 * g : 512 * g + 512].rearrange("p (t m) -> p t m", t=4), in_=ps[:].rearrange("p (m t) -> p t m", t=4), func=ACT.Tanh, scale=0.5)
+            ps = rot_tile()
+            mm(ps[:], X["z", "q"], wq, vpl, 4, 512 * g, 512)
+            X["q", g] = ps
+
+        def q_tanh(g):
+            nc.scalar.activation(out=tm(tq[:, 512 * g : 512 * g + 512]), in_=mt(X["q", g][:]), func=ACT.Tanh, scale=0.5)
 
         def q_T(g):
-            ps = num_pool.tile([P, 512], F32, name="num%d" % g, tag="num%d" % g)
+            ps = misc_tile()
             for t in range(4):
                 c = slice(128 * t, 128 * t + 128)
                 nc.tensor.transpose(ps[:, c], tq[:, 512 * g + 128 * t : 512 * g + 128 * t + 128], ident[:])
-            nc.scalar.activation(out=tT[g][:].rearrange("p (b t) -> p b t", t=4), in_=ps[:].rearrange("p (t b) -> p b t", t=4), func=ACT.Copy, bias=1.0)
+            X["qt", g] = ps
 
-        ep = {}
+        def q_out(g):
+            nc.scalar.activation(out=bt(tT[g][:]), in_=tb(X["qt", g][:]), func=ACT.Copy, bias=1.0)
+
+        def den_tile(g):
+            X["d", g] = num_pool.tile([P, 512], F32, name="d%d" % (g % 2), tag="d%d" % (g % 2))
+
+        def den_turn(g, src, c0, first, last):
+            for t in range(4):
+                nc.tensor.matmul(X["d", g][:, 128 * t : 128 * t + 128], lhsT=src[:, c0 + 128 * t : c0 + 128 * t + 128], rhs=ident[:], start=(first and t == 0), stop=(last and t == 3), is_transpose=True)
+
+        def U(w, g):
+            if w == 0:
+                den_tile(g)
+            den_turn(g, X["e", w], 512 * g, w == 0, w == W - 1)
 
         def D_T(g):
-            if g % 2:
-                ps = rot_pool.tile([P, 512], F32, name="rot", tag="rot")
-            else:
-                ps = misc_pool.tile([P, 512], F32, name="misc", tag="misc")
-            srcs = [den] + [e[w] for w in PE_DEN]
-            for i in range(len(srcs)):
-                for t in range(4):
-                    c0 = 512 * g + 128 * t
-                    nc.tensor.matmul(ps[:, 128 * t : 128 * t + 128], lhsT=srcs[i][:, c0 : c0 + 128], rhs=ident[:], start=(i == 0 and t == 0), stop=(i == len(srcs) - 1 and t == 3), is_transpose=True)
+            den_tile(g)
+            den_turn(g, den, 512 * g - 1024, True, False)
+            for w in PE_DEN:
+                den_turn(g, X["e", w], 512 * g, False, w == PE_DEN[-1])
+
+        def root(g):
             s = work.tile([P, 512], F32, name="rs", tag="rs")
-            nc.scalar.activation(out=s[:].rearrange("p (b t) -> p b t", t=4), in_=ps[:].rearrange("p (t b) -> p b t", t=4), func=ACT.Abs_reciprocal_sqrt, bias=2.0 * EPS, scale=2.0)
+            nc.scalar.activation(out=bt(s[:]), in_=tb(X["d", g][:]), func=ACT.Abs_reciprocal_sqrt, bias=2.0 * EPS, scale=2.0)
+            X["s", g] = s
+
+        def sq(g, vec=False):
             r = work.tile([P, 512], F32, name="rr", tag="rr")
-            nc.scalar.activation(out=r[:], in_=s[:], func=ACT.Square)
-            ep["r", g] = r
-            c = keep.tile([P, 512], F32, name="cc%d" % g)
-            nc.gpsimd.tensor_tensor(out=c[:], in0=tT[g][:], in1=r[:], op=ALU.mult)
-            ep["m", g] = c
+            if vec:
+                nc.vector.tensor_tensor(out=r[:], in0=X["s", g][:], in1=X["s", g][:], op=ALU.mult)
+            else:
+                nc.scalar.activation(out=r[:], in_=X["s", g][:], func=ACT.Square)
+            X["r", g] = r
+
+        def n2(g):
+            t = work.tile([P, 512], F32, name="n2", tag="n2")
+            nc.vector.tensor_tensor(out=bt(t[:]), in0=bt(tT[g][:]), in1=tb(num[g][:]), op=ALU.mult)
+            X["n", g] = t
 
         def h_v(g):
             t = work.tile([P, 512], BF16, name="hh", tag="hh", align_bytes=64)
-            nc.vector.tensor_tensor(
-                out=t[:].rearrange("p (b t) -> p b t", t=4),
-                in0=ep["m", g][:].rearrange("p (b t) -> p b t", t=4),
-                in1=num[g][:].rearrange("p (t b) -> p b t", t=4),
-                op=ALU.mult,
-            )
-            ep["h", g] = t
+            nc.vector.tensor_tensor(out=t[:], in0=X["n", g][:], in1=X["r", g][:], op=ALU.mult)
+            X["h", g] = t
 
         def h_q(g):
-            c = work.tile([P, 128], U32, name="hc", tag="hc", align_bytes=64)
-            s = work.tile([P, 128], U8, name="hs", tag="hs", align_bytes=64)
-            nc.vector.quantize_mx(out=c[:].bitcast(FP8X4), scales=s[:], in_=ep["h", g][:])
-            ep["c", g] = (c[:], s[:])
+            c = keep.tile([P, 128], U32, name="hc%d" % g, align_bytes=64)
+            s = keep.tile([P, 128], U8, name="hs%d" % g, align_bytes=64)
+            nc.vector.quantize_mx(out=c[:].bitcast(FP8X4), scales=s[:], in_=X["h", g][:])
+            X["hc", g] = (c[:], s[:])
 
-        def o_mm(g):
-            for i in range(2):
-                if g == 0:
-                    ep["o", i] = num_pool.tile([P, 512], F32, name="num%d" % i, tag="num%d" % i)
-                mm(ep["o", i][:, 0:256], ep["c", g], wo, vpl, 8, 512 * g + 256 * i, 256, start=(g == 0), stop=(g == G - 1))
+        def o_mm(g, i):
+            if g == 0:
+                X["o", i] = misc_tile() if i == 0 else num_pool.tile([P, 512], F32, name="d0", tag="d0")
+            mm(X["o", i][:, 0:256], X["hc", g], wo, vpl, 8, 512 * g + 256 * i, 256, start=(g == 0), stop=(g == G - 1))
 
-        LAG = 3
-        GSET = {}
-        z_widen([0], "v")
-        z_turn([0])
-        z_widen([1], "s")
-        z_scale([0])
-        z_quant([0])
-        z_turn([1])
-        z_widen([2, 3], "s")
-        z_scale([1])
-        z_quant([1])
+        o_sb = [keep.tile([P, 256], F32, name="o_sb%d" % i) for i in range(2)]
 
-        steps = []
-        for s in range(W + LAG):
-            pw = s - LAG
-            ks = [("k", s, g) for g in range(G)] if s < W else []
-            ps = [("g" if (pw, g) in GSET else "p", pw, g) for g in range(G)] if pw >= 0 else []
-            gs = [u for u in ps if u[0] == "g"]
-            ps = [u for u in ps if u[0] == "p"]
-            units = list(gs)
-            if s == W - 1:
-                units += ks + ps
+        def o_out(i):
+            if i == 0:
+                nc.vector.tensor_copy(out=o_sb[i][:], in_=X["o", i][:, 0:256])
             else:
-                for g in range(G):
-                    units += ks[g : g + 1] + ps[g : g + 1]
-            steps.append(units)
-        flat = [u for st in steps for u in st]
+                nc.scalar.copy(out=o_sb[i][:], in_=X["o", i][:, 0:256])
+            nc.sync.dma_start(out=out[:, 256 * i : 256 * i + 256], in_=o_sb[i][:])
 
-        def fill(i):
-            if i < len(flat):
-                kind, w, g = flat[i]
-                if kind == "k":
-                    K_mm(w, g)
-                else:
-                    P_mm(w, g)
+        seq = PARAM.get("order", "k0 k1 a0 k2 a1 k3 q0 a2 k4 q1 a3 k5 q2 a4 k6 q3 a5 k7 a6 b0 a7 b1 b2 b3 b4 b5 b6 b7").split()
+        gset = [tuple(u) for u in PARAM.get("gset", ())]
+        flat = []
+        for o in seq:
+            if o[0] == "q":
+                flat.append(("q", 0, int(o[1])))
+            else:
+                for g in {"k": (0, 1, 2, 3), "a": (0, 1), "b": (2, 3)}[o[0]]:
+                    flat.append(("k" if o[0] == "k" else "p", int(o[1]), g))
+        idx = {flat[i]: i for i in range(len(flat))}
+        acts = []
 
-        turns = []
+        def at(name, pos, fn, *args):
+            if "log" in PARAM:
+                PARAM["log"][name] = pos
+            acts.append((PARAM.get(name, pos), len(acts), fn, args, name))
 
-        def T_flush(n):
-            for i in range(min(n, len(turns))):
-                T(*turns.pop(0))
+        for i in range(len(flat)):
+            kind, w, g = flat[i]
+            fill = {"k": (K_mm, w, g), "p": (P_mm, w, g), "q": (q_mm, g)}[kind]
+            at("fill%d" % i, i - LOOK - 0.5, *fill)
+            if kind == "k":
+                at("use%d" % i, i, K_copy, w, g)
+            elif kind == "q":
+                at("use%d" % i, i, q_tanh, g)
+            elif (w, g) in gset:
+                at("vs%d_%d" % (w, g), i, P_s, w, g)
+                at("vg%d_%d" % (w, g), i, P_g, w, g)
+            else:
+                at("use%d" % i, i, P_v, w, g)
+        kb = [idx["k", w, 0] for w in range(W)]
 
-        for i in range(LOOK):
-            fill(i)
-        pos = 0
-        for s in range(W + LAG):
-            st = steps[s]
-            for j in range(len(st)):
-                fill(pos + LOOK)
-                pos += 1
-                kind, w, g = st[j]
-                if kind == "k":
-                    K_copy(w, g)
-                elif kind == "p":
-                    P_v(w, g)
-                else:
-                    P_g(w, g)
-                key = kind + str(g)
-                jj = j - len([u for u in st if u[0] == "g"])
-                if jj == 0 and 1 <= s < W:
-                    M_a(s - 1)
-                if jj == 1 and 1 <= s < W:
-                    M_b(s - 1)
-                    E(s - 1, 2)
-                    D(s - 1)
-                if s == W - 1 and jj == 4:
-                    M_a(s)
-                if s == W - 1 and jj == 5:
-                    M_b(s)
-                    E(s, 4)
-                    D(s)
-                    nc.scalar.activation(out=dummy[:], in_=one[:], func=ACT.Abs_reciprocal_sqrt)
-                for zs, zw in ((0, 2), (1, 4), (2, 6)):
-                    if s == zs:
-                        if key == "k1":
-                            if zw < 6:
-                                z_widen([zw + 2, zw + 3], "s")
-                            z_turn([zw, zw + 1])
-                        if key == "k2":
-                            z_scale([zw, zw + 1])
-                        if key == "k3":
-                            z_quant([zw, zw + 1])
-                if s == 0 and key == "k2":
-                    q_turn()
-                if s == 1 and key == "k0":
-                    q_quant()
-                if s == 2:
-                    if key == "k1":
-                        q_mm(0)
-                    if key == "k2":
-                        q_mm(1)
-                        q_mm(2)
-                    if key == "k3":
-                        q_mm(3)
-                        q_T(0)
-                if s == 3:
-                    if jj == 1:
-                        q_T(1)
-                        q_T(2)
-                        q_T(3)
-                if kind != "k":
-                    if not (pos >= len(flat) - 3):
-                        turns.append((w, g))
-                if len(turns) > 2 and s < W + LAG - 1:
-                    T_flush(2)
-                if s == W + LAG - 2 and key == "p3":
-                    D_T(0)
-                if s == W + LAG - 1:
-                    if key == "p0":
-                        T_flush(9)
-                        D_T(1)
-                        T(7, 0)
-                        D_T(2)
-                    if key == "p1":
-                        T(7, 1)
-                        D_T(3)
-                    if key == "p2":
-                        h_v(0)
-                        T(7, 2)
-                    if key == "p3":
-                        h_q(0)
-                        h_v(1)
-                        T(7, 3)
-                        h_q(1)
-                        h_v(2)
-                        o_mm(0)
-                        o_mm(1)
-                        h_q(2)
-                        h_v(3)
-                        h_q(3)
-                        o_mm(2)
-                        o_mm(3)
-        o_sb = keep.tile([P, 256], F32, name="o_sb")
-        o_sb2 = keep.tile([P, 256], F32, name="o_sb2")
-        nc.vector.tensor_copy(out=o_sb[:], in_=ep["o", 0][:, 0:256])
-        nc.sync.dma_start(out=out[:, 0:256], in_=o_sb[:])
-        nc.scalar.copy(out=o_sb2[:], in_=ep["o", 1][:, 0:256])
-        nc.sync.dma_start(out=out[:, 256:512], in_=o_sb2[:])
+        at("zw0", -9.0, z_widen, 0, 1, True)
+        at("zt0", -8.9, z_turn, 0, 1)
+        at("zw1", -8.8, z_widen, 1, 1)
+        at("zs0", -8.7, z_scale, 0, 1)
+        if len(ZV) < 4:
+            at("spt", -8.6, spread_turn)
+            at("spc", -8.5, spread_copy)
+        at("zq0", -8.4, z_quant, 0, 1)
+        for w, n, p0, p1, p2 in ((1, 1, -8.2, 0.1, 1.1), (2, 2, -8.1, 3.1, 5.1), (4, 2, 0.4, kb[2] + 0.1, kb[2] + 3.1), (6, 2, 3.4, kb[3] + 0.1, kb[3] + 3.1)):
+            if w > 1:
+                at("zw%d" % w, p0 - 0.1, z_widen, w, n)
+            if w not in ZV:
+                at("zm%d" % w, p0, z_mul, w, n)
+            at("zt%d" % w, p1, z_turn, w, n)
+            at("zc%d" % w, p1 + 0.1, z_scale if w in ZV else z_copy, w, n)
+            at("zq%d" % w, p2, z_quant, w, n)
+        at("ztq", kb[2] + 1.1, q_turn)
+        at("zcq", kb[2] + 1.2, z_copy, "q", 1)
+        at("zqq", kb[2] + 3.2, z_quant, "q", 1)
+        for w in range(W):
+            b = kb[w] + 4
+            at("mv%d" % w, b + 0.10, M_v, w)
+            at("mp%d" % w, b + 0.11, M_pe, w)
+            at("mb%d" % w, b + 1.20, M_b, w)
+            for i in range(2):
+                at("e%d_%d" % (w, i), b + 1.21 + 0.01 * i, E, w, i, 2)
+            if w >= 1 and w not in PE_DEN:
+                at("d%d" % w, b + 1.25, D, w)
+            for g in range(2):
+                at("u%d_%d" % (w, g), idx["p", w, 1] + 4.2 if w < W - 2 else idx["p", w, 0] + 0.2, U, w, g)
+        at("tab", kb[7] + 5.3, nc.scalar.activation, dummy[:], one[:], ACT.Abs_reciprocal_sqrt)
+        for w in range(W):
+            for g in range(G):
+                i = idx["p", w, g]
+                at("t%d_%d" % (w, g), i + 4.3 if g < 2 and w < W - 1 else max(i + 0.3, idx["p", 7, 1] + (0.6 if g > 1 else 0.3)), T, w, g)
+        for g in range(G):
+            i = idx["q", 0, g]
+            at("qt%d" % g, i + 3.4, q_T, g)
+            at("qo%d" % g, i + 3.5, q_out, g)
+        n = len(flat)
+        for g in range(G):
+            b = idx["p", 7, 1] + 0.5 + g * 0.01 if g < 2 else n + g
+            r = b if g < 2 else n - 8 + 4 * (g - 2)
+            if g >= 2:
+                at("dt%d" % g, r, D_T, g)
+            at("ro%d" % g, r + 0.001, root, g)
+            at("sq%d" % g, r + 0.002, sq, g)
+            at("n2_%d" % g, b, n2, g)
+            at("h%d" % g, b + 2, h_v, g)
+            at("hq%d" % g, b + 3, h_q, g)
+            for i in range(2):
+                at("om%d_%d" % (g, i), n - 1 + g + 0.1 * i if g < 2 else b + 3.1 + 0.01 * i, o_mm, g, i)
+        for i in range(2):
+            at("oo%d" % i, n + 20 + i, o_out, i)
+        acts.sort(key=lambda a: (a[0], a[1]))
+        for a in acts:
+            if "marks" in PARAM:
+                PARAM["marks"].append((a[4], PARAM["cnt"]()))
+            a[2](*a[3])

@@ -21,306 +21,292 @@ EPS = 1e-8
 FLOPS = 2 * B * L * A * (1 + 2 * W) + 2 * B * A * L
 LOOK = 2
 PARAM = {
-    "zv": [1],
-    "pe_den": [6,7],
-    "zw0": 0,
-    "zt0": 1,
-    "zw1": 3,
-    "zs0": 2,
-    "spt": 4,
-    "spc": 9,
-    "zq0": 5,
-    "zw2": 6,
-    "zm2": 15,
+    "zv": [1,2],
+    "pe_den": [7],
+    "zw0": 1,
+    "zt0": 3,
+    "zw1": 5,
+    "zs0": 4,
+    "zq0": 6,
+    "spt": 0,
+    "spc": 2,
+    "zw2": 8,
     "fill0": 7,
-    "fill1": 16,
-    "fill2": 11,
-    "use0": 8,
-    "zt1": 13,
-    "zc1": 19,
-    "zw4": 14,
-    "zm4": 26,
-    "fill3": 10,
+    "zw4": 17,
+    "zm4": 24,
+    "zw6": 22,
+    "zm6": 36,
+    "fill1": 14,
+    "fill2": 16,
+    "zt1": 9,
+    "fill3": 18,
+    "use0": 10,
+    "zc1": 11,
+    "zq1": 13,
+    "fill4": 19,
+    "zt2": 12,
     "use1": 20,
-    "zq1": 22,
-    "fill4": 25,
-    "use2": 17,
-    "fill5": 28,
-    "use3": 12,
-    "zt2": 30,
-    "zc2": 33,
-    "zw6": 18,
-    "zm6": 38,
-    "fill6": 29,
-    "use4": 27,
-    "mv0": 24,
-    "mp0": 35,
-    "fill7": 32,
-    "use5": 31,
-    "zq2": 36,
+    "fill5": 25,
+    "use2": 23,
+    "zc2": 15,
+    "fill6": 27,
+    "use3": 29,
+    "zq2": 31,
+    "fill7": 30,
+    "zt4": 35,
+    "use4": 26,
+    "zc4": 50,
+    "mv0": 32,
+    "mp0": 34,
+    "fill8": 40,
+    "use5": 33,
     "mb0": 37,
-    "e0_0": 50,
-    "e0_1": 41,
-    "fill8": 52,
-    "use6": 34,
-    "fill9": 53,
-    "use7": 40,
-    "fill10": 39,
-    "use8": 57,
+    "e0_0": 39,
+    "e0_1": 44,
+    "fill9": 42,
+    "use6": 38,
+    "zq4": 54,
+    "fill10": 46,
+    "use7": 41,
+    "fill11": 43,
+    "zt6": 51,
+    "use8": 45,
+    "zc6": 56,
     "mv1": 47,
-    "mp1": 55,
-    "fill11": 42,
-    "use9": 59,
-    "mb1": 62,
-    "e1_0": 73,
-    "e1_1": 65,
-    "d1": 76,
-    "fill12": 45,
-    "use10": 44,
-    "zt4": 43,
-    "zc4": 46,
-    "fill13": 49,
-    "use11": 48,
+    "mp1": 53,
+    "fill12": 49,
+    "use9": 48,
+    "zq6": 62,
+    "mb1": 57,
+    "e1_0": 60,
+    "e1_1": 67,
+    "d1": 72,
+    "fill13": 55,
+    "use10": 52,
+    "fill14": 58,
+    "use11": 59,
     "ztq": 21,
-    "zcq": 23,
-    "fill14": 74,
-    "use12": 51,
-    "t0_0": 60,
-    "fill15": 79,
-    "use13": 54,
-    "zq4": 66,
-    "zqq": 63,
-    "u0_0": 58,
-    "u0_1": 56,
-    "t0_1": 67,
-    "fill16": 61,
-    "use14": 82,
-    "mv2": 68,
-    "mp2": 70,
-    "fill17": 64,
-    "use15": 84,
-    "mb2": 72,
-    "e2_0": 80,
-    "e2_1": 89,
-    "d2": 96,
-    "fill18": 71,
-    "use16": 69,
-    "zt6": 77,
-    "zc6": 85,
-    "fill19": 81,
-    "use17": 75,
-    "fill20": 99,
-    "use18": 78,
-    "t1_0": 86,
-    "fill21": 88,
+    "zcq": 28,
+    "fill15": 63,
+    "use12": 65,
+    "zqq": 64,
+    "fill16": 70,
+    "use13": 69,
+    "fill17": 73,
+    "use14": 71,
+    "fill18": 75,
+    "use15": 74,
+    "mv2": 76,
+    "mp2": 79,
+    "t0_0": 66,
+    "t0_1": 61,
+    "t0_2": 68,
+    "fill19": 78,
+    "use16": 77,
+    "mb2": 83,
+    "e2_0": 85,
+    "e2_1": 90,
+    "d2": 97,
+    "fill20": 81,
+    "use17": 80,
+    "fill21": 82,
+    "use18": 84,
+    "fill22": 88,
     "use19": 87,
-    "zq6": 91,
-    "u1_0": 92,
-    "u1_1": 83,
-    "t1_1": 95,
-    "fill22": 90,
-    "use20": 102,
-    "mv3": 93,
-    "mp3": 97,
-    "fill23": 103,
-    "use21": 94,
-    "mb3": 101,
-    "e3_0": 106,
-    "e3_1": 111,
-    "d3": 118,
-    "fill24": 100,
-    "use22": 98,
-    "fill25": 109,
-    "use23": 108,
-    "qt0": 107,
-    "fill26": 110,
-    "qo0": 117,
-    "use24": 104,
-    "fill27": 113,
-    "use25": 112,
-    "t2_0": 105,
-    "fill28": 116,
-    "use26": 115,
-    "u2_0": 123,
-    "u2_1": 119,
-    "t2_1": 114,
-    "fill29": 125,
-    "use27": 122,
-    "mv4": 120,
-    "mp4": 124,
-    "fill30": 127,
-    "use28": 121,
-    "mb4": 126,
-    "e4_0": 128,
-    "e4_1": 134,
-    "d4": 141,
-    "fill31": 130,
-    "use29": 129,
-    "fill32": 133,
-    "use30": 132,
-    "qt1": 131,
-    "fill33": 136,
-    "qo1": 140,
-    "use31": 135,
-    "fill34": 139,
-    "use32": 138,
-    "t3_0": 137,
-    "fill35": 145,
-    "use33": 143,
-    "u3_0": 150,
-    "u3_1": 142,
-    "t3_1": 153,
-    "fill36": 146,
-    "use34": 144,
-    "mv5": 147,
-    "mp5": 152,
-    "fill37": 149,
-    "use35": 148,
-    "mb5": 154,
-    "e5_0": 157,
-    "e5_1": 162,
-    "d5": 169,
-    "fill38": 156,
-    "use36": 151,
-    "fill39": 158,
-    "use37": 155,
-    "qt2": 160,
-    "fill40": 161,
-    "qo2": 168,
-    "use38": 159,
-    "fill41": 172,
-    "use39": 163,
-    "t4_0": 167,
-    "fill42": 176,
-    "use40": 166,
-    "u4_0": 165,
-    "u4_1": 171,
-    "t4_1": 178,
-    "fill43": 164,
-    "use41": 175,
-    "mv6": 173,
-    "mp6": 179,
-    "fill44": 174,
-    "use42": 180,
-    "mb6": 183,
-    "e6_0": 191,
-    "e6_1": 185,
-    "fill45": 182,
-    "use43": 170,
-    "fill46": 184,
-    "use44": 177,
-    "qt3": 188,
-    "fill47": 187,
-    "qo3": 197,
-    "use45": 186,
-    "fill48": 192,
-    "use46": 189,
-    "t5_0": 190,
-    "fill49": 194,
-    "use47": 193,
-    "u5_0": 181,
-    "u5_1": 195,
-    "t5_1": 199,
-    "fill50": 200,
-    "use48": 201,
-    "mv7": 196,
-    "mp7": 202,
-    "u6_0": 203,
-    "u6_1": 205,
-    "fill51": 208,
-    "use49": 198,
-    "mb7": 204,
-    "e7_0": 212,
-    "e7_1": 207,
-    "tab": 218,
-    "fill52": 215,
-    "use50": 206,
-    "fill53": 217,
-    "use51": 210,
-    "fill54": 209,
-    "use52": 220,
-    "u7_0": 221,
-    "u7_1": 223,
-    "t6_0": 213,
-    "fill55": 211,
-    "use53": 222,
-    "t6_1": 219,
-    "t7_0": 225,
-    "t7_1": 226,
-    "fill56": 228,
-    "n2_0": 227,
-    "ro0": 224,
-    "sq0": 237,
-    "n2_1": 229,
-    "ro1": 234,
-    "sq1": 240,
-    "t0_2": 231,
-    "t0_3": 233,
-    "use54": 214,
-    "t1_2": 235,
-    "fill57": 230,
-    "use55": 216,
-    "t1_3": 239,
-    "fill58": 242,
-    "h0": 241,
-    "h1": 244,
-    "use56": 232,
-    "t2_2": 238,
-    "fill59": 243,
-    "hq0": 255,
-    "hq1": 249,
-    "use57": 236,
-    "t2_3": 246,
-    "fill60": 245,
-    "use58": 247,
-    "t3_2": 252,
-    "fill61": 256,
-    "use59": 250,
-    "t3_3": 254,
-    "fill62": 258,
-    "use60": 251,
-    "dt2": 248,
-    "ro2": 253,
-    "sq2": 257,
-    "t4_2": 261,
-    "fill63": 260,
-    "use61": 262,
-    "t4_3": 265,
-    "fill64": 267,
-    "use62": 259,
-    "t5_2": 271,
-    "fill65": 274,
-    "use63": 264,
-    "t5_3": 273,
-    "fill66": 268,
-    "use64": 269,
-    "dt3": 263,
-    "ro3": 266,
-    "sq3": 270,
-    "t6_2": 277,
-    "fill67": 275,
-    "use65": 276,
-    "t6_3": 280,
-    "use66": 272,
-    "t7_2": 279,
-    "use67": 278,
-    "om0_0": 283,
-    "om0_1": 285,
-    "t7_3": 282,
-    "om1_0": 286,
-    "om1_1": 287,
-    "n2_2": 281,
-    "n2_3": 284,
-    "h2": 288,
-    "hq2": 290,
-    "h3": 289,
-    "om2_0": 292,
-    "om2_1": 294,
-    "hq3": 291,
-    "om3_0": 293,
-    "om3_1": 295,
-    "oo0": 296,
-    "oo1": 297,
+    "fill23": 89,
+    "use20": 91,
+    "fill24": 94,
+    "use21": 93,
+    "fill25": 98,
+    "use22": 95,
+    "fill26": 99,
+    "use23": 96,
+    "mv3": 100,
+    "mp3": 103,
+    "t1_0": 86,
+    "t1_1": 105,
+    "t1_2": 92,
+    "fill27": 102,
+    "use24": 101,
+    "mb3": 107,
+    "e3_0": 109,
+    "e3_1": 114,
+    "d3": 125,
+    "fill28": 106,
+    "use25": 104,
+    "fill29": 110,
+    "use26": 108,
+    "fill30": 111,
+    "use27": 112,
+    "fill31": 116,
+    "use28": 115,
+    "fill32": 118,
+    "use29": 117,
+    "fill33": 122,
+    "use30": 119,
+    "fill34": 127,
+    "use31": 121,
+    "mv4": 124,
+    "mp4": 130,
+    "qt0": 113,
+    "qo0": 123,
+    "t2_0": 120,
+    "t2_1": 131,
+    "t2_2": 133,
+    "fill35": 136,
+    "use32": 126,
+    "mb4": 132,
+    "e4_0": 135,
+    "e4_1": 141,
+    "d4": 154,
+    "fill36": 128,
+    "use33": 134,
+    "fill37": 138,
+    "use34": 129,
+    "fill38": 139,
+    "use35": 140,
+    "fill39": 142,
+    "use36": 137,
+    "fill40": 145,
+    "use37": 144,
+    "fill41": 148,
+    "use38": 146,
+    "fill42": 150,
+    "use39": 147,
+    "mv5": 151,
+    "mp5": 155,
+    "qt1": 143,
+    "qo1": 149,
+    "t3_0": 157,
+    "t3_1": 162,
+    "t3_2": 159,
+    "fill43": 153,
+    "use40": 152,
+    "mb5": 158,
+    "e5_0": 161,
+    "e5_1": 166,
+    "d5": 184,
+    "fill44": 164,
+    "use41": 156,
+    "fill45": 165,
+    "use42": 160,
+    "fill46": 168,
+    "use43": 163,
+    "fill47": 169,
+    "use44": 167,
+    "fill48": 171,
+    "use45": 170,
+    "fill49": 175,
+    "use46": 172,
+    "fill50": 179,
+    "use47": 174,
+    "mv6": 177,
+    "mp6": 183,
+    "qt2": 173,
+    "qo2": 176,
+    "t4_0": 186,
+    "t4_1": 187,
+    "t4_2": 190,
+    "fill51": 180,
+    "use48": 178,
+    "mb6": 188,
+    "e6_0": 195,
+    "e6_1": 191,
+    "d6": 212,
+    "fill52": 182,
+    "use49": 181,
+    "fill53": 192,
+    "use50": 185,
+    "fill54": 196,
+    "use51": 189,
+    "fill55": 198,
+    "use52": 193,
+    "fill56": 194,
+    "use53": 197,
+    "fill57": 210,
+    "use54": 202,
+    "mv7": 205,
+    "mp7": 207,
+    "qt3": 199,
+    "qo3": 203,
+    "t5_0": 208,
+    "t5_1": 201,
+    "t5_2": 204,
+    "fill58": 213,
+    "use55": 206,
+    "mb7": 209,
+    "e7_0": 211,
+    "e7_1": 218,
+    "tab": 224,
+    "fill59": 215,
+    "use56": 200,
+    "fill60": 216,
+    "use57": 214,
+    "fill61": 219,
+    "use58": 217,
+    "fill62": 227,
+    "use59": 221,
+    "t6_0": 220,
+    "t6_1": 222,
+    "t6_2": 225,
+    "dt0": 236,
+    "ro0": 240,
+    "sq0": 248,
+    "fill63": 228,
+    "use60": 223,
+    "dt1": 246,
+    "ro1": 251,
+    "sq1": 255,
+    "fill64": 230,
+    "use61": 226,
+    "fill65": 231,
+    "use62": 229,
+    "fill66": 233,
+    "use63": 232,
+    "dt2": 254,
+    "ro2": 259,
+    "sq2": 263,
+    "fill67": 242,
+    "use64": 235,
+    "t7_0": 234,
+    "t7_1": 239,
+    "t7_2": 241,
+    "n2_0": 238,
+    "t0_3": 243,
+    "t1_3": 244,
+    "t2_3": 250,
+    "t3_3": 252,
+    "use65": 237,
+    "h0": 249,
+    "n2_1": 253,
+    "dt3": 262,
+    "ro3": 267,
+    "sq3": 271,
+    "use66": 245,
+    "hq0": 256,
+    "h1": 257,
+    "n2_2": 261,
+    "use67": 247,
+    "hq1": 264,
+    "h2": 265,
+    "t4_3": 258,
+    "t5_3": 260,
+    "t6_3": 266,
+    "hq2": 269,
+    "t7_3": 268,
+    "om0_0": 270,
+    "om0_1": 274,
+    "om1_0": 273,
+    "om1_1": 275,
+    "om2_0": 276,
+    "om2_1": 277,
+    "n2_3": 272,
+    "h3": 278,
+    "hq3": 279,
+    "om3_0": 280,
+    "om3_1": 281,
+    "oo0": 282,
+    "oo1": 283,
 }
 
 
@@ -331,25 +317,25 @@ def tile_aftblock_pa_w8_kernel(tc, z_current, z_window_bytes, z_window_scale, Wq
     with ExitStack() as ctx:
         keep = ctx.enter_context(tc.tile_pool(name="keep", bufs=1))
         work = ctx.enter_context(tc.tile_pool(name="work", bufs=2))
-        ev_pool = ctx.enter_context(tc.tile_pool(name="evp", bufs=4))
+        late_pool = ctx.enter_context(tc.tile_pool(name="late", bufs=6))
         num_pool = ctx.enter_context(tc.psum_pool(name="nump", bufs=1))
-        rot_pool = ctx.enter_context(tc.psum_pool(name="rotp", bufs=3))
+        rot_pool = ctx.enter_context(tc.psum_pool(name="rotp", bufs=4))
         misc_pool = ctx.enter_context(tc.psum_pool(name="miscp", bufs=1))
         ctx.enter_context(tc.manual_schedule())
 
         ident = keep.tile([P, P], F32, name="ident")
         one = keep.tile([P, 1], F32, name="one")
-        wk = keep.tile([P, A], U32, name="wk", align_bytes=64)
-        wv = keep.tile([P, A], U32, name="wv", align_bytes=64)
-        wq = keep.tile([P, A], U32, name="wq", align_bytes=64)
-        wo = keep.tile([P, A], U32, name="wo", align_bytes=64)
-        kpl = keep.tile([P, A], U8, name="kpl", align_bytes=64)
-        vpl = keep.tile([P, A], U8, name="vpl", align_bytes=64)
+        wk = keep.tile([P, A], U32, name="wk", align_bytes=256)
+        wv = keep.tile([P, A], U32, name="wv", align_bytes=256)
+        wq = keep.tile([P, A], U32, name="wq", align_bytes=256)
+        wo = keep.tile([P, A], U32, name="wo", align_bytes=256)
+        kpl = keep.tile([P, A], U8, name="kpl", align_bytes=256)
+        vpl = keep.tile([P, A], U8, name="vpl", align_bytes=256)
         ZCUT = (0, 1, 4, 8)
         zby = [keep.tile([P, ZCUT[i + 1] - ZCUT[i], L], U8, name="zby%d" % i, align_bytes=64) for i in range(3)]
         sc = keep.tile([P, 4], F32, name="sc")
         zq_in = keep.tile([P, L], BF16, name="zq_in", align_bytes=64)
-        den = keep.tile([P, 1024], F32, name="den")
+        den = keep.tile([P, A], F32, name="den")
         nm = keep.tile([P, W], F32, name="nm")
         tq = keep.tile([P, A], F32, name="tq")
         tT = [keep.tile([P, 512], F32, name="tT%d" % g) for g in range(G)]
@@ -357,12 +343,12 @@ def tile_aftblock_pa_w8_kernel(tc, z_current, z_window_bytes, z_window_scale, Wq
         nc.vector.memset(kpl[:].bitcast(U32), 0)
         nc.vector.memset(one[:], 1.0)
         nc.vector.memset(vpl[:].bitcast(U32), 0)
-        nc.gpsimd.dma_start(out=sc[:], in_=z_window_scale.rearrange("o c (p t) -> p (o c t)", t=4))
         make_identity(nc, ident[:])
 
         def load_z(i):
             nc.sync.dma_start(out=zby[i][:], in_=z_window_bytes[ZCUT[i] : ZCUT[i + 1]].rearrange("w b k -> b w k"))
 
+        nc.sync.dma_start(out=sc[:], in_=z_window_scale.rearrange("o c (p t) -> p (o c t)", t=4))
         load_z(0)
 
         def load_scales(tile, k, src):
@@ -382,9 +368,10 @@ def tile_aftblock_pa_w8_kernel(tc, z_current, z_window_bytes, z_window_scale, Wq
         load_scales(vpl, 4, Wq_scales[0])
         for q in range(4):
             nc.sync.dma_start(out=vpl[32 * q + 8 : 32 * q + 12, :].bitcast(I32).rearrange("p (g n) -> p g n", g=G), in_=Wo_scales.bitcast(I32)[:, 4 * q : 4 * q + 4, :].rearrange("g q n -> q g n"))
-        for tl, src in ((wv, Wv_words), (wq, Wq_words)):
-            for h in range(2):
-                load_words(tl, src[0], 1024 * h, 1024 * h + 1024)
+        for h in range(2):
+            load_words(wv, Wv_words[0], 1024 * h, 1024 * h + 1024)
+        for h in range(2):
+            load_words(wq, Wq_words[0], 1024 * h, 1024 * h + 1024)
         nc.sync.dma_start(out=wo[:].bitcast(I32).rearrange("p (g n) -> p g n", g=G), in_=Wo_words.rearrange("g p n t -> p g (n t)").bitcast(I32))
 
         dummy = keep.tile([P, 1], F32, name="dummy")
@@ -440,8 +427,11 @@ def tile_aftblock_pa_w8_kernel(tc, z_current, z_window_bytes, z_window_scale, Wq
             nc.gpsimd.tensor_tensor(out=t[:], in0=X["zb", w][:], in1=scb[:].unsqueeze(1).to_broadcast([P, n, L]), op=ALU.mult)
             X["zt", w] = t
 
+        def acc_tile(i):
+            return num_pool.tile([P, 512], F32, name="n%d" % i, tag="n%d" % i)
+
         def z_turn(w, n):
-            ps = misc_tile()
+            ps = misc_tile() if w == 0 else acc_tile({1: 0, 2: 1, 4: 2, 6: 0}[w])
             for i in range(n):
                 words = X["zt", w][:, i, :].bitcast(F32)
                 for u in range(2):
@@ -465,14 +455,14 @@ def tile_aftblock_pa_w8_kernel(tc, z_current, z_window_bytes, z_window_scale, Wq
             X["zg", w] = t
 
         def z_quant(w, n):
-            c = keep.tile([P, 128 * n], U32, name="zc%s" % w, align_bytes=64)
-            s = keep.tile([P, 128 * n], U8, name="zs%s" % w, align_bytes=64)
+            c = keep.tile([P, 128 * n], U32, name="zc%s" % w, align_bytes=256)
+            s = keep.tile([P, 128 * n], U8, name="zs%s" % w, align_bytes=256)
             nc.vector.quantize_mx(out=c[:].bitcast(FP8X4), scales=s[:], in_=X["zg", w][:])
             for i in range(n):
                 X["z", w if w == "q" else w + i] = (c[:, 128 * i : 128 * i + 128], s[:, 128 * i : 128 * i + 128])
 
         def spread_turn():
-            ps = misc_tile()
+            ps = acc_tile(2)
             for t in range(4):
                 nc.tensor.transpose(ps[:, 128 * t : 128 * t + 128], sc[:, t : t + 1].to_broadcast([P, P]), ident[:])
             X["sp"] = ps
@@ -487,7 +477,7 @@ def tile_aftblock_pa_w8_kernel(tc, z_current, z_window_bytes, z_window_scale, Wq
 
         def K_copy(w, g):
             if ("nk", w) not in X:
-                X["nk", w] = keep.tile([P, A], F32, name="nk%d" % (w % 4), tag="nk%d" % (w % 4))
+                X["nk", w] = keep.tile([P, A], F32, name="nk%d" % (w % 3), tag="nk%d" % (w % 3))
                 X["mn", w] = work.tile([P, G], F32, name="mn", tag="mn")
             nc.vector.tensor_scalar(
                 out=tm(X["nk", w][:, 512 * g : 512 * g + 512]),
@@ -518,8 +508,9 @@ def tile_aftblock_pa_w8_kernel(tc, z_current, z_window_bytes, z_window_scale, Wq
             n = A // parts
             nc.scalar.activation(out=X["e", w][:, n * i : n * i + n], in_=X["nk", w][:, n * i : n * i + n], func=ACT.Exp, bias=nm[:, w : w + 1], scale=-1.0)
 
-        def D(w):
-            nc.gpsimd.tensor_tensor(out=den[:], in0=X["e", 0][:, 1024:] if w == 1 else den[:], in1=X["e", w][:, 1024:], op=ALU.add)
+        def D(w, c0=0, c1=A):
+            c = slice(c0, c1)
+            nc.gpsimd.tensor_tensor(out=den[:, c], in0=X["e", 0][:, c] if w == 1 else den[:, c], in1=X["e", w][:, c], op=ALU.add)
 
         num = [None] * G
 
@@ -529,7 +520,7 @@ def tile_aftblock_pa_w8_kernel(tc, z_current, z_window_bytes, z_window_scale, Wq
             X["v", w, g] = ps
 
         def P_v(w, g):
-            t = ev_pool.tile([P, 512], F32, name="ev%d" % (g % 2), tag="ev%d" % (g % 2))
+            t = (late_pool if g == 3 else work).tile([P, 512], F32, name="ev%d" % g, tag="ev%d" % g)
             nc.vector.tensor_tensor(out=tm(t[:]), in0=tm(X["e", w][:, 512 * g : 512 * g + 512]), in1=mt(X["v", w, g][:]), op=ALU.mult)
             X["ev", w, g] = t
 
@@ -539,19 +530,19 @@ def tile_aftblock_pa_w8_kernel(tc, z_current, z_window_bytes, z_window_scale, Wq
             X["vs", w, g] = v
 
         def P_g(w, g):
-            t = ev_pool.tile([P, 512], F32, name="ev%d" % (g % 2), tag="ev%d" % (g % 2))
+            t = (late_pool if g == 3 else work).tile([P, 512], F32, name="ev%d" % g, tag="ev%d" % g)
             nc.gpsimd.tensor_tensor(out=t[:], in0=X["e", w][:, 512 * g : 512 * g + 512], in1=X["vs", w, g][:], op=ALU.mult)
             X["ev", w, g] = t
 
         def T(w, g):
             if w == 0:
-                num[g] = num_pool.tile([P, 512], F32, name="n%d" % (g % 2), tag="n%d" % (g % 2))
+                num[g] = num_pool.tile([P, 512], F32, name="n%d" % (g % 3), tag="n%d" % (g % 3))
             for t in range(4):
                 c = slice(128 * t, 128 * t + 128)
                 nc.tensor.matmul(num[g][:, c], lhsT=X["ev", w, g][:, c], rhs=ident[:], start=(w == 0 and t == 0), stop=(w == W - 1 and t == 3), is_transpose=True)
 
         def q_turn():
-            ps = misc_tile()
+            ps = acc_tile(1)
             words = zq_in[:].bitcast(F32)
             for u in range(2):
                 nc.tensor.transpose(ps[:, u * 128 : u * 128 + 128], words[:, u : 256 : 2], ident[:])
@@ -575,23 +566,14 @@ def tile_aftblock_pa_w8_kernel(tc, z_current, z_window_bytes, z_window_scale, Wq
         def q_out(g):
             nc.scalar.activation(out=bt(tT[g][:]), in_=tb(X["qt", g][:]), func=ACT.Copy, bias=1.0)
 
-        def den_tile(g):
-            X["d", g] = num_pool.tile([P, 512], F32, name="d%d" % (g % 2), tag="d%d" % (g % 2))
-
-        def den_turn(g, src, c0, first, last):
-            for t in range(4):
-                nc.tensor.matmul(X["d", g][:, 128 * t : 128 * t + 128], lhsT=src[:, c0 + 128 * t : c0 + 128 * t + 128], rhs=ident[:], start=(first and t == 0), stop=(last and t == 3), is_transpose=True)
-
-        def U(w, g):
-            if w == 0:
-                den_tile(g)
-            den_turn(g, X["e", w], 512 * g, w == 0, w == W - 1)
-
         def D_T(g):
-            den_tile(g)
-            den_turn(g, den, 512 * g - 1024, True, False)
-            for w in PE_DEN:
-                den_turn(g, X["e", w], 512 * g, False, w == PE_DEN[-1])
+            ps = misc_tile()
+            srcs = [den] + [X["e", w] for w in PE_DEN]
+            for i in range(len(srcs)):
+                for t in range(4):
+                    c0 = 512 * g + 128 * t
+                    nc.tensor.matmul(ps[:, 128 * t : 128 * t + 128], lhsT=srcs[i][:, c0 : c0 + 128], rhs=ident[:], start=(i == 0 and t == 0), stop=(i == len(srcs) - 1 and t == 3), is_transpose=True)
+            X["d", g] = ps
 
         def root(g):
             s = work.tile([P, 512], F32, name="rs", tag="rs")
@@ -624,7 +606,7 @@ def tile_aftblock_pa_w8_kernel(tc, z_current, z_window_bytes, z_window_scale, Wq
 
         def o_mm(g, i):
             if g == 0:
-                X["o", i] = misc_tile() if i == 0 else num_pool.tile([P, 512], F32, name="d0", tag="d0")
+                X["o", i] = num_pool.tile([P, 512], F32, name="n%d" % (1 + i), tag="n%d" % (1 + i))
             mm(X["o", i][:, 0:256], X["hc", g], wo, vpl, 8, 512 * g + 256 * i, 256, start=(g == 0), stop=(g == G - 1))
 
         o_sb = [keep.tile([P, 256], F32, name="o_sb%d" % i) for i in range(2)]
@@ -636,14 +618,14 @@ def tile_aftblock_pa_w8_kernel(tc, z_current, z_window_bytes, z_window_scale, Wq
                 nc.scalar.copy(out=o_sb[i][:], in_=X["o", i][:, 0:256])
             nc.sync.dma_start(out=out[:, 256 * i : 256 * i + 256], in_=o_sb[i][:])
 
-        seq = PARAM.get("order", "k0 k1 a0 k2 a1 k3 q0 a2 k4 q1 a3 k5 q2 a4 k6 q3 a5 k7 a6 b0 a7 b1 b2 b3 b4 b5 b6 b7").split()
+        seq = PARAM.get("order", "k0 k1 a0 k2 a1 k3 q0 a2 k4 q1 a3 k5 q2 a4 k6 q3 a5 k7 a6 b0 b1 a7 b2 b3 b4 b5 b6 b7").split()
         gset = [tuple(u) for u in PARAM.get("gset", ())]
         flat = []
         for o in seq:
             if o[0] == "q":
                 flat.append(("q", 0, int(o[1])))
             else:
-                for g in {"k": (0, 1, 2, 3), "a": (0, 1), "b": (2, 3)}[o[0]]:
+                for g in {"k": (0, 1, 2, 3), "a": (0, 1, 2), "b": (3,)}[o[0]]:
                     flat.append(("k" if o[0] == "k" else "p", int(o[1]), g))
         idx = {flat[i]: i for i in range(len(flat))}
         acts = []
@@ -653,10 +635,11 @@ def tile_aftblock_pa_w8_kernel(tc, z_current, z_window_bytes, z_window_scale, Wq
                 PARAM["log"][name] = pos
             acts.append((PARAM.get(name, pos), len(acts), fn, args, name))
 
+        LK = PARAM.get("look", 3)
         for i in range(len(flat)):
             kind, w, g = flat[i]
             fill = {"k": (K_mm, w, g), "p": (P_mm, w, g), "q": (q_mm, g)}[kind]
-            at("fill%d" % i, i - LOOK - 0.5, *fill)
+            at("fill%d" % i, i - LK - 0.5, *fill)
             if kind == "k":
                 at("use%d" % i, i, K_copy, w, g)
             elif kind == "q":
@@ -672,54 +655,68 @@ def tile_aftblock_pa_w8_kernel(tc, z_current, z_window_bytes, z_window_scale, Wq
         at("zt0", -8.9, z_turn, 0, 1)
         at("zw1", -8.8, z_widen, 1, 1)
         at("zs0", -8.7, z_scale, 0, 1)
-        if len(ZV) < 4:
-            at("spt", -8.6, spread_turn)
-            at("spc", -8.5, spread_copy)
         at("zq0", -8.4, z_quant, 0, 1)
-        for w, n, p0, p1, p2 in ((1, 1, -8.2, 0.1, 1.1), (2, 2, -8.1, 3.1, 5.1), (4, 2, 0.4, kb[2] + 0.1, kb[2] + 3.1), (6, 2, 3.4, kb[3] + 0.1, kb[3] + 3.1)):
+        if len(ZV) < 4:
+            at("spt", -8.3, spread_turn)
+            at("spc", -8.2, spread_copy)
+        for w, n, p0, p1, p2, p3 in ((1, 1, -8.6, -1.4, 0.05, 0.1), (2, 2, -4.1, 0.6, 2.1, 3.1), (4, 2, -3.0, 3.6, 4.1, 6.1), (6, 2, -2.9, 7.6, 8.1, 9.1)):
             if w > 1:
                 at("zw%d" % w, p0 - 0.1, z_widen, w, n)
             if w not in ZV:
                 at("zm%d" % w, p0, z_mul, w, n)
             at("zt%d" % w, p1, z_turn, w, n)
-            at("zc%d" % w, p1 + 0.1, z_scale if w in ZV else z_copy, w, n)
-            at("zq%d" % w, p2, z_quant, w, n)
-        at("ztq", kb[2] + 1.1, q_turn)
-        at("zcq", kb[2] + 1.2, z_copy, "q", 1)
-        at("zqq", kb[2] + 3.2, z_quant, "q", 1)
+            at("zc%d" % w, p2 if w != 1 else 0.05, z_scale if w in ZV else z_copy, w, n)
+            at("zq%d" % w, p3, z_quant, w, n)
+        at("ztq", kb[2] + 0.1, q_turn)
+        at("zcq", kb[2] + 0.2, z_copy, "q", 1)
+        at("zqq", kb[2] + 1.2, z_quant, "q", 1)
+        p0 = [idx["k", 1, 0]] + [idx["p", w - 1, 0] for w in range(1, W)]
+        oM = PARAM.get("oM", (0.1, 1.1))
+        oR = PARAM.get("oR", (0.2, 0.2, 0.2, 0.2, 0.2, 0.2, 0.2, 0.2, 0.2, 3.2))
+        run = {}
         for w in range(W):
-            b = kb[w] + 4
-            at("mv%d" % w, b + 0.10, M_v, w)
-            at("mp%d" % w, b + 0.11, M_pe, w)
-            at("mb%d" % w, b + 1.20, M_b, w)
+            b = p0[w]
+            x = b + oR[w]
+            at("mv%d" % w, b + oM[0], M_v, w)
+            run[w] = [("mp%d" % w, M_pe, w)]
+            at("mb%d" % w, b + oM[1], M_b, w)
             for i in range(2):
-                at("e%d_%d" % (w, i), b + 1.21 + 0.01 * i, E, w, i, 2)
+                at("e%d_%d" % (w, i), b + oM[1] + 0.01 + 0.01 * i, E, w, i, 2)
             if w >= 1 and w not in PE_DEN:
-                at("d%d" % w, b + 1.25, D, w)
-            for g in range(2):
-                at("u%d_%d" % (w, g), idx["p", w, 1] + 4.2 if w < W - 2 else idx["p", w, 0] + 0.2, U, w, g)
-        at("tab", kb[7] + 5.3, nc.scalar.activation, dummy[:], one[:], ACT.Abs_reciprocal_sqrt)
+                if w < W - 1:
+                    at("d%d" % w, b + oM[1] + 0.05, D, w)
+                else:
+                    for i in range(4):
+                        at("d7_%d" % i, b + oM[1] + 0.05 + 0.01 * i, D, w, 512 * i, 512 * i + 512)
+        at("tab", p0[7] + oM[1] + 0.1, nc.scalar.activation, dummy[:], one[:], ACT.Abs_reciprocal_sqrt)
+        for g in range(G):
+            w = PARAM.get("qrun", (4, 5, 6, 7))[g]
+            run[w] += [("qt%d" % g, q_T, g), ("qo%d" % g, q_out, g)]
+        run[8] = []
+        run[9] = []
         for w in range(W):
-            for g in range(G):
-                i = idx["p", w, g]
-                at("t%d_%d" % (w, g), i + 4.3 if g < 2 and w < W - 1 else max(i + 0.3, idx["p", 7, 1] + (0.6 if g > 1 else 0.3)), T, w, g)
-        for g in range(G):
-            i = idx["q", 0, g]
-            at("qt%d" % g, i + 3.4, q_T, g)
-            at("qo%d" % g, i + 3.5, q_out, g)
+            for g in range(3):
+                run[w + 2] += [("t%d_%d" % (w, g), T, w, g)]
+        p0 += [idx["p", 7, 0], idx["p", 7, 2]]
+        for w in range(10):
+            for j in range(len(run[w])):
+                at(run[w][j][0], p0[w] + oR[w] + 0.001 * j, *run[w][j][1:])
+        oL = PARAM.get("oL", (0.5, 3.5))
+        for w in range(W):
+            at("t%d_3" % w, max(idx["p", w, 3] + 1.4, p0[9] + oR[9] + oL[0] + (oL[1] if w > PARAM.get("oLw", 3) else 0)) + 0.001 * w, T, w, 3)
         n = len(flat)
+        e0 = p0[9] + oR[9]
         for g in range(G):
-            b = idx["p", 7, 1] + 0.5 + g * 0.01 if g < 2 else n + g
-            r = b if g < 2 else n - 8 + 4 * (g - 2)
-            if g >= 2:
-                at("dt%d" % g, r, D_T, g)
+            r = PARAM.get("oDT", (p0[8] + 0.3, p0[8] + 1.3, p0[9] + 2.3, p0[9] + 4.3))[g]
+            at("dt%d" % g, r, D_T, g)
             at("ro%d" % g, r + 0.001, root, g)
             at("sq%d" % g, r + 0.002, sq, g)
+            b = e0 + PARAM.get("oN2", 0.05) + g * 1.0 if g < 3 else n + 4
             at("n2_%d" % g, b, n2, g)
-            at("h%d" % g, b + 2, h_v, g)
-            at("hq%d" % g, b + 3, h_q, g)
+            at("h%d" % g, b + PARAM.get("oH", 1.0), h_v, g)
+            at("hq%d" % g, b + PARAM.get("oH", 1.0) + 1.0, h_q, g)
             for i in range(2):
-                at("om%d_%d" % (g, i), n - 1 + g + 0.1 * i if g < 2 else b + 3.1 + 0.01 * i, o_mm, g, i)
+                at("om%d_%d" % (g, i), max(b + PARAM.get("oH", 1.0) + 1.1, e0 + 4.5 + 0.1 * g) + 0.01 * i, o_mm, g, i)
         for i in range(2):
             at("oo%d" % i, n + 20 + i, o_out, i)
         acts.sort(key=lambda a: (a[0], a[1]))

@@ -16,711 +16,444 @@ AX = mybir.AxisListType
 
 P = 128
 B, L, A, W = 128, 512, 2048, 8
-G = A // 512
+Q = 512
+G = A // Q
 EPS = 1e-8
 FLOPS = 2 * B * L * A * (1 + 2 * W) + 2 * B * A * L
-LOOK = 2
-PARAM = {
-    "zv": [1,2],
-    "pe_den": [7],
-    "zw0": 1,
-    "zt0": 3,
-    "zw1": 5,
-    "zs0": 4,
-    "zq0": 6,
-    "spt": 0,
-    "spc": 2,
-    "zw2": 8,
-    "fill0": 7,
-    "zw4": 17,
-    "zm4": 24,
-    "zw6": 22,
-    "zm6": 36,
-    "fill1": 14,
-    "fill2": 16,
-    "zt1": 9,
-    "fill3": 18,
-    "use0": 10,
-    "zc1": 11,
-    "zq1": 13,
-    "fill4": 19,
-    "zt2": 12,
-    "use1": 20,
-    "fill5": 25,
-    "use2": 23,
-    "zc2": 15,
-    "fill6": 27,
-    "use3": 29,
-    "zq2": 31,
-    "fill7": 30,
-    "zt4": 35,
-    "use4": 26,
-    "zc4": 50,
-    "mv0": 32,
-    "mp0": 34,
-    "fill8": 40,
-    "use5": 33,
-    "mb0": 37,
-    "e0_0": 39,
-    "e0_1": 44,
-    "fill9": 42,
-    "use6": 38,
-    "zq4": 54,
-    "fill10": 46,
-    "use7": 41,
-    "fill11": 43,
-    "zt6": 51,
-    "use8": 45,
-    "zc6": 56,
-    "mv1": 47,
-    "mp1": 53,
-    "fill12": 49,
-    "use9": 48,
-    "zq6": 62,
-    "mb1": 57,
-    "e1_0": 60,
-    "e1_1": 67,
-    "d1": 72,
-    "fill13": 55,
-    "use10": 52,
-    "fill14": 58,
-    "use11": 59,
-    "ztq": 21,
-    "zcq": 28,
-    "fill15": 63,
-    "use12": 65,
-    "zqq": 64,
-    "fill16": 70,
-    "use13": 69,
-    "fill17": 73,
-    "use14": 71,
-    "fill18": 75,
-    "use15": 74,
-    "mv2": 76,
-    "mp2": 79,
-    "t0_0": 66,
-    "t0_1": 61,
-    "t0_2": 68,
-    "fill19": 78,
-    "use16": 77,
-    "mb2": 83,
-    "e2_0": 85,
-    "e2_1": 90,
-    "d2": 97,
-    "fill20": 81,
-    "use17": 80,
-    "fill21": 82,
-    "use18": 84,
-    "fill22": 88,
-    "use19": 87,
-    "fill23": 89,
-    "use20": 91,
-    "fill24": 94,
-    "use21": 93,
-    "fill25": 98,
-    "use22": 95,
-    "fill26": 99,
-    "use23": 96,
-    "mv3": 100,
-    "mp3": 103,
-    "t1_0": 86,
-    "t1_1": 105,
-    "t1_2": 92,
-    "fill27": 102,
-    "use24": 101,
-    "mb3": 107,
-    "e3_0": 109,
-    "e3_1": 114,
-    "d3": 125,
-    "fill28": 106,
-    "use25": 104,
-    "fill29": 110,
-    "use26": 108,
-    "fill30": 111,
-    "use27": 112,
-    "fill31": 116,
-    "use28": 115,
-    "fill32": 118,
-    "use29": 117,
-    "fill33": 122,
-    "use30": 119,
-    "fill34": 127,
-    "use31": 121,
-    "mv4": 124,
-    "mp4": 130,
-    "qt0": 113,
-    "qo0": 123,
-    "t2_0": 120,
-    "t2_1": 131,
-    "t2_2": 133,
-    "fill35": 136,
-    "use32": 126,
-    "mb4": 132,
-    "e4_0": 135,
-    "e4_1": 141,
-    "d4": 154,
-    "fill36": 128,
-    "use33": 134,
-    "fill37": 138,
-    "use34": 129,
-    "fill38": 139,
-    "use35": 140,
-    "fill39": 142,
-    "use36": 137,
-    "fill40": 145,
-    "use37": 144,
-    "fill41": 148,
-    "use38": 146,
-    "fill42": 150,
-    "use39": 147,
-    "mv5": 151,
-    "mp5": 155,
-    "qt1": 143,
-    "qo1": 149,
-    "t3_0": 157,
-    "t3_1": 162,
-    "t3_2": 159,
-    "fill43": 153,
-    "use40": 152,
-    "mb5": 158,
-    "e5_0": 161,
-    "e5_1": 166,
-    "d5": 184,
-    "fill44": 164,
-    "use41": 156,
-    "fill45": 165,
-    "use42": 160,
-    "fill46": 168,
-    "use43": 163,
-    "fill47": 169,
-    "use44": 167,
-    "fill48": 171,
-    "use45": 170,
-    "fill49": 175,
-    "use46": 172,
-    "fill50": 179,
-    "use47": 174,
-    "mv6": 177,
-    "mp6": 183,
-    "qt2": 173,
-    "qo2": 176,
-    "t4_0": 186,
-    "t4_1": 187,
-    "t4_2": 190,
-    "fill51": 180,
-    "use48": 178,
-    "mb6": 188,
-    "e6_0": 195,
-    "e6_1": 191,
-    "d6": 212,
-    "fill52": 182,
-    "use49": 181,
-    "fill53": 192,
-    "use50": 185,
-    "fill54": 196,
-    "use51": 189,
-    "fill55": 198,
-    "use52": 193,
-    "fill56": 194,
-    "use53": 197,
-    "fill57": 210,
-    "use54": 202,
-    "mv7": 205,
-    "mp7": 207,
-    "qt3": 199,
-    "qo3": 203,
-    "t5_0": 208,
-    "t5_1": 201,
-    "t5_2": 204,
-    "fill58": 213,
-    "use55": 206,
-    "mb7": 209,
-    "e7_0": 211,
-    "e7_1": 218,
-    "tab": 224,
-    "fill59": 215,
-    "use56": 200,
-    "fill60": 216,
-    "use57": 214,
-    "fill61": 219,
-    "use58": 217,
-    "fill62": 227,
-    "use59": 221,
-    "t6_0": 220,
-    "t6_1": 222,
-    "t6_2": 225,
-    "dt0": 236,
-    "ro0": 240,
-    "sq0": 248,
-    "fill63": 228,
-    "use60": 223,
-    "dt1": 246,
-    "ro1": 251,
-    "sq1": 255,
-    "fill64": 230,
-    "use61": 226,
-    "fill65": 231,
-    "use62": 229,
-    "fill66": 233,
-    "use63": 232,
-    "dt2": 254,
-    "ro2": 259,
-    "sq2": 263,
-    "fill67": 242,
-    "use64": 235,
-    "t7_0": 234,
-    "t7_1": 239,
-    "t7_2": 241,
-    "n2_0": 238,
-    "t0_3": 243,
-    "t1_3": 244,
-    "t2_3": 250,
-    "t3_3": 252,
-    "use65": 237,
-    "h0": 249,
-    "n2_1": 253,
-    "dt3": 262,
-    "ro3": 267,
-    "sq3": 271,
-    "use66": 245,
-    "hq0": 256,
-    "h1": 257,
-    "n2_2": 261,
-    "use67": 247,
-    "hq1": 264,
-    "h2": 265,
-    "t4_3": 258,
-    "t5_3": 260,
-    "t6_3": 266,
-    "hq2": 269,
-    "t7_3": 268,
-    "om0_0": 270,
-    "om0_1": 274,
-    "om1_0": 273,
-    "om1_1": 275,
-    "om2_0": 276,
-    "om2_1": 277,
-    "n2_3": 272,
-    "h3": 278,
-    "hq3": 279,
-    "om3_0": 280,
-    "om3_1": 281,
-    "oo0": 282,
-    "oo1": 283,
+
+WINDOW_CUTS = (0, 1, 4, 8)
+
+TURN = (
+    ("value_mm", 2, 2),
+    ("exponential", 0, 1),
+    ("key_mm", 0, 0),
+    ("weigh", 3, 2),
+    ("key_mm", 1, 0),
+    ("key_mm", 3, 0),
+    ("weigh", 2, 2),
+    ("key_copy", 0, 0),
+    ("gate_mm", 0, 3),
+    ("add_turned", 3, 3),
+    ("add_turned", 1, 2),
+    ("add_denominator", 0, 2),
+    ("exponential", 1, 1),
+    ("key_copy", 1, 0),
+    ("key_mm", 2, 0),
+    ("value_mm", 0, 1),
+    ("gate_exp", 0, 3),
+    ("gate_plus_one", 0, 4),
+    ("value_mm", 1, 1),
+    ("value_mm", 3, 1),
+    ("key_copy", 3, 0),
+    ("key_copy", 2, 0),
+    ("weigh", 0, 1),
+    ("row_minimum", 0, 0),
+    ("weigh", 1, 1),
+    ("add_turned", 2, 2),
+    ("turn_minimum", 0, 0),
+    ("add_turned", 0, 1),
+    ("step_minimum", 0, 0),
+)
+TURNS = W + 1
+
+PREPARE = {
+    (0, "key_mm", 1): (("z_widen", 2), ("z_turn", 1)),
+    (0, "key_copy", 1): (("z_scale", 1),),
+    (0, "value_mm", 0): (("z_turn", 2), ("z_widen", 6)),
+    (0, "gate_exp", 0): (("z_quantise", 1),),
+    (0, "turn_minimum", 0): (("z_scale", 2),),
+    (1, "key_mm", 0): (("z_widen", 4),),
+    (1, "value_mm", 3): (("z_turn", "q"), ("z_multiply", 6)),
+    (1, "key_copy", 2): (("z_quantise", 2), ("z_turn", 6)),
+    (1, "turn_minimum", 0): (("z_copy", "q"),),
+    (2, "key_copy", 0): (("z_multiply", 4),),
+    (2, "add_turned", 3): (("z_quantise", "q"),),
+    (2, "add_denominator", 0): (("z_turn", 4),),
+    (2, "value_mm", 0): (("z_copy", 4),),
+    (3, "add_denominator", 0): (("z_copy", 6),),
+    (3, "gate_plus_one", 0): (("z_quantise", 6), ("z_quantise", 4)),
 }
+GROUP = {0: 1, 1: 1, 2: 2, 4: 2, 6: 2, "q": 1}
+SCALED_LATE = (0, 1, 2)
+VECTOR_HELPS = (2, 4)
+TURNED_IN = {0: 3, 1: 0, 2: 1, 4: 2, 6: 3, "q": 0}
+
+
+def grouped(ap):
+    return ap.rearrange("p (t m) -> p t m", t=4)
+
+
+def natural(ap):
+    return ap.rearrange("p (m t) -> p t m", t=4)
 
 
 def tile_aftblock_pa_w8_kernel(tc, z_current, z_window_bytes, z_window_scale, Wq_words, Wq_scales, Wk_words, Wk_scales, Wv_words, Wv_scales, Wo_words, Wo_scales, out):
     nc = tc.nc
-    PE_DEN = PARAM.get("pe_den", (7,))
-    ZV = PARAM.get("zv", ())
     with ExitStack() as ctx:
         keep = ctx.enter_context(tc.tile_pool(name="keep", bufs=1))
-        work = ctx.enter_context(tc.tile_pool(name="work", bufs=2))
-        late_pool = ctx.enter_context(tc.tile_pool(name="late", bufs=6))
-        num_pool = ctx.enter_context(tc.psum_pool(name="nump", bufs=1))
-        rot_pool = ctx.enter_context(tc.psum_pool(name="rotp", bufs=4))
-        misc_pool = ctx.enter_context(tc.psum_pool(name="miscp", bufs=1))
+        pair = ctx.enter_context(tc.tile_pool(name="pair", bufs=2))
+        triple = ctx.enter_context(tc.tile_pool(name="triple", bufs=3))
+        sum_pool = ctx.enter_context(tc.psum_pool(name="sums", bufs=1))
+        bank_pool = ctx.enter_context(tc.psum_pool(name="banks", bufs=4))
         ctx.enter_context(tc.manual_schedule())
+
+        def sum_bank(i):
+            return sum_pool.tile([P, Q], F32, name="sum%d" % i, tag="sum%d" % i)
+
+        def bank():
+            return bank_pool.tile([P, Q], F32, name="bank", tag="bank")
 
         ident = keep.tile([P, P], F32, name="ident")
         one = keep.tile([P, 1], F32, name="one")
-        wk = keep.tile([P, A], U32, name="wk", align_bytes=256)
-        wv = keep.tile([P, A], U32, name="wv", align_bytes=256)
-        wq = keep.tile([P, A], U32, name="wq", align_bytes=256)
-        wo = keep.tile([P, A], U32, name="wo", align_bytes=256)
-        kpl = keep.tile([P, A], U8, name="kpl", align_bytes=256)
-        vpl = keep.tile([P, A], U8, name="vpl", align_bytes=256)
-        ZCUT = (0, 1, 4, 8)
-        zby = [keep.tile([P, ZCUT[i + 1] - ZCUT[i], L], U8, name="zby%d" % i, align_bytes=64) for i in range(3)]
-        sc = keep.tile([P, 4], F32, name="sc")
-        zq_in = keep.tile([P, L], BF16, name="zq_in", align_bytes=64)
+        table = keep.tile([P, 1], F32, name="table")
+
+        k_words = keep.tile([P, A], U32, name="k_words", align_bytes=256)
+        v_words = keep.tile([P, A], U32, name="v_words", align_bytes=256)
+        q_words = keep.tile([P, A], U32, name="q_words", align_bytes=256)
+        o_words = keep.tile([P, A], U32, name="o_words", align_bytes=256)
+        k_scales = keep.tile([P, A], U8, name="k_scales", align_bytes=256)
+        v_scales = keep.tile([P, A], U8, name="v_scales", align_bytes=256)
+        qo_scales = keep.tile([P, A], U8, name="qo_scales", align_bytes=256)
+        q_row, o_row = 0, 4
+
+        z_bytes = [keep.tile([P, WINDOW_CUTS[i + 1] - WINDOW_CUTS[i], L], U8, name="z_bytes%d" % i, align_bytes=64) for i in range(3)]
+        zc = keep.tile([P, L], BF16, name="zc", align_bytes=64)
+        z_scales = keep.tile([P, 4], F32, name="z_scales")
+        z_scales_wide = keep.tile([P, L], F32, name="z_scales_wide")
+
+        weights = [keep.tile([P, A], F32, name="weights%d" % w) for w in range(W)]
+        shift = keep.tile([P, W], F32, name="shift")
         den = keep.tile([P, A], F32, name="den")
-        nm = keep.tile([P, W], F32, name="nm")
-        tq = keep.tile([P, A], F32, name="tq")
-        tT = [keep.tile([P, 512], F32, name="tT%d" % g) for g in range(G)]
+        exp_q = keep.tile([P, A], F32, name="exp_q")
+        gate_den = keep.tile([P, A], F32, name="gate_den")
 
-        nc.vector.memset(kpl[:].bitcast(U32), 0)
+        nc.vector.memset(k_scales[:].bitcast(U32), 0)
         nc.vector.memset(one[:], 1.0)
-        nc.vector.memset(vpl[:].bitcast(U32), 0)
+        nc.vector.memset(v_scales[:].bitcast(U32), 0)
         make_identity(nc, ident[:])
+        nc.gpsimd.memset(qo_scales[:].bitcast(U32), 0)
 
-        def load_z(i):
-            nc.sync.dma_start(out=zby[i][:], in_=z_window_bytes[ZCUT[i] : ZCUT[i + 1]].rearrange("w b k -> b w k"))
+        def load_window(i):
+            nc.sync.dma_start(out=z_bytes[i][:], in_=z_window_bytes[WINDOW_CUTS[i] : WINDOW_CUTS[i + 1]].rearrange("w b k -> b w k"))
 
-        nc.sync.dma_start(out=sc[:], in_=z_window_scale.rearrange("o c (p t) -> p (o c t)", t=4))
-        load_z(0)
-
-        def load_scales(tile, k, src):
-            for q in range(4):
-                nc.sync.dma_start(out=tile[32 * q + k : 32 * q + k + 4, :].bitcast(I32), in_=src[4 * q : 4 * q + 4, :].bitcast(I32))
+        def load_scales(tile, row, src):
+            for r in range(4):
+                nc.sync.dma_start(out=tile[32 * r + row : 32 * r + row + 4, :].bitcast(I32), in_=src[4 * r : 4 * r + 4, :].bitcast(I32))
 
         def load_words(tile, src, c0, c1):
             nc.sync.dma_start(out=tile[:, c0:c1].bitcast(I32), in_=src.rearrange("p n t -> p (n t)")[:, 4 * c0 : 4 * c1].bitcast(I32))
 
-        load_scales(kpl, 0, Wk_scales[0])
-        load_words(wk, Wk_words[0], 0, 512)
-        load_z(1)
-        load_words(wk, Wk_words[0], 512, 2048)
-        load_z(2)
-        nc.sync.dma_start(out=zq_in[:], in_=z_current)
-        load_scales(vpl, 0, Wv_scales[0])
-        load_scales(vpl, 4, Wq_scales[0])
-        for q in range(4):
-            nc.sync.dma_start(out=vpl[32 * q + 8 : 32 * q + 12, :].bitcast(I32).rearrange("p (g n) -> p g n", g=G), in_=Wo_scales.bitcast(I32)[:, 4 * q : 4 * q + 4, :].rearrange("g q n -> q g n"))
-        for h in range(2):
-            load_words(wv, Wv_words[0], 1024 * h, 1024 * h + 1024)
-        for h in range(2):
-            load_words(wq, Wq_words[0], 1024 * h, 1024 * h + 1024)
-        nc.sync.dma_start(out=wo[:].bitcast(I32).rearrange("p (g n) -> p g n", g=G), in_=Wo_words.rearrange("g p n t -> p g (n t)").bitcast(I32))
+        nc.sync.dma_start(out=z_scales[:], in_=z_window_scale.rearrange("o c (p t) -> p (o c t)", t=4))
+        load_window(0)
+        load_scales(k_scales, 0, Wk_scales[0])
+        load_words(k_words, Wk_words[0], 0, 512)
+        load_window(1)
+        load_words(k_words, Wk_words[0], 512, 1024)
+        load_words(k_words, Wk_words[0], 1024, 2048)
+        load_window(2)
+        load_scales(v_scales, 0, Wv_scales[0])
+        for half in (0, 1024):
+            load_words(v_words, Wv_words[0], half, half + 1024)
+        nc.sync.dma_start(out=zc[:], in_=z_current)
+        load_scales(qo_scales, q_row, Wq_scales[0])
+        for half in (0, 1024):
+            load_words(q_words, Wq_words[0], half, half + 1024)
+        for r in range(4):
+            nc.sync.dma_start(
+                out=qo_scales[32 * r + o_row : 32 * r + o_row + 4, :].bitcast(I32).rearrange("p (g n) -> p g n", g=G),
+                in_=Wo_scales.bitcast(I32)[:, 4 * r : 4 * r + 4, :].rearrange("g q n -> q g n"),
+            )
+        nc.sync.dma_start(out=o_words[:].bitcast(I32).rearrange("p (g n) -> p g n", g=G), in_=Wo_words.rearrange("g p n t -> p g (n t)").bitcast(I32))
 
-        dummy = keep.tile([P, 1], F32, name="dummy")
-        nc.scalar.activation(out=dummy[:], in_=one[:], func=ACT.Exp)
+        nc.scalar.activation(out=table[:], in_=one[:], func=ACT.Exp)
 
-        def mm(ps, code, w_tile, plane, k, c0, n, start=True, stop=True):
+        def mx(ps, stationary, words, scales, row, c0, n, start=True, stop=True):
+            codes, bytes_of_codes = stationary
             nc.tensor.matmul_mx(
                 out=ps,
-                lhsT=code[0].bitcast(FP8X4),
-                lhsT_scale=code[1],
-                rhs=w_tile[:, c0 : c0 + n].bitcast(FP8X4),
-                rhs_scale=plane[k:P, c0 : c0 + n],
+                lhsT=codes.bitcast(FP8X4),
+                lhsT_scale=bytes_of_codes,
+                rhs=words[:, c0 : c0 + n].bitcast(FP8X4),
+                rhs_scale=scales[row:P, c0 : c0 + n],
                 start=start,
                 stop=stop,
             )
 
-        def tm(ap):
-            return ap.rearrange("p (t m) -> p t m", t=4)
+        wide = {}
+        turned = {}
+        z4 = {}
+        z_mx = {}
+        wide["q"] = zc[:].unsqueeze(1)
 
-        def mt(ap):
-            return ap.rearrange("p (m t) -> p t m", t=4)
-
-        def bt(ap):
-            return ap.rearrange("p (b t) -> p b t", t=4)
-
-        def tb(ap):
-            return ap.rearrange("p (t b) -> p b t", t=4)
-
-        X = {}
-
-        def rot_tile():
-            return rot_pool.tile([P, 512], F32, name="rot", tag="rot")
-
-        def misc_tile():
-            return misc_pool.tile([P, 512], F32, name="misc", tag="misc")
-
-        scb = keep.tile([P, L], F32, name="scb")
-
-        def z_widen(w, n, vec=False):
-            t = keep.tile([P, n, L], BF16, name="zb%d" % w, align_bytes=64)
-            i = max(i for i in range(3) if ZCUT[i] <= w)
-            src = zby[i][:, w - ZCUT[i] : w - ZCUT[i] + n, :].bitcast(FP8)
-            if vec:
+        def z_widen(s):
+            n = GROUP[s]
+            t = keep.tile([P, n, L], BF16, name="wide%d" % s, align_bytes=64)
+            i = max(i for i in range(3) if WINDOW_CUTS[i] <= s)
+            src = z_bytes[i][:, s - WINDOW_CUTS[i] : s - WINDOW_CUTS[i] + n, :].bitcast(FP8)
+            if s == 0:
                 nc.vector.tensor_copy(out=t[:], in_=src)
             else:
                 nc.scalar.copy(out=t[:], in_=src)
-            X["zb", w] = t
-            if vec or w in ZV:
-                X["zt", w] = t
+            wide[s] = t
 
-        def z_mul(w, n):
-            t = keep.tile([P, n, L], BF16, name="zm%d" % w, align_bytes=64)
-            nc.gpsimd.tensor_tensor(out=t[:], in0=X["zb", w][:], in1=scb[:].unsqueeze(1).to_broadcast([P, n, L]), op=ALU.mult)
-            X["zt", w] = t
+        def turn_scales():
+            ps = sum_bank(2)
+            for t in range(4):
+                nc.tensor.transpose(ps[:, 128 * t : 128 * t + 128], z_scales[:, t : t + 1].to_broadcast([P, P]), ident[:])
+            nc.scalar.copy(out=z_scales_wide[:].rearrange("p (u m e) -> p u m e", u=2, e=2), in_=ps[:].rearrange("p (u e m) -> p u m e", u=2, e=2))
 
-        def acc_tile(i):
-            return num_pool.tile([P, 512], F32, name="n%d" % i, tag="n%d" % i)
+        def z_multiply(s):
+            t = keep.tile([P, GROUP[s], L], BF16, name="product%d" % s, align_bytes=64)
+            for i in range(GROUP[s]):
+                nc.gpsimd.tensor_tensor(
+                    out=t[:, i, :].rearrange("p (u m e) -> p u m e", u=2, e=2),
+                    in0=wide[s][:, i, :].rearrange("p (m u e) -> p u m e", u=2, e=2),
+                    in1=z_scales_wide[:].rearrange("p (u m e) -> p u m e", u=2, e=2),
+                    op=ALU.mult,
+                )
+            wide[s] = t
 
-        def z_turn(w, n):
-            ps = misc_tile() if w == 0 else acc_tile({1: 0, 2: 1, 4: 2, 6: 0}[w])
+        def z_turn(s):
+            n = GROUP[s]
+            ps = sum_bank(TURNED_IN[s])
             for i in range(n):
-                words = X["zt", w][:, i, :].bitcast(F32)
+                words = wide[s][:, i, :].bitcast(F32)
                 for u in range(2):
-                    nc.tensor.transpose(ps[:, u * 128 * n + i * 128 : u * 128 * n + i * 128 + 128], words[:, u : 256 : 2], ident[:])
-            X["zp", w] = ps
+                    src = words[:, u:256:2] if s == "q" or s in SCALED_LATE else words[:, 128 * u : 128 * u + 128]
+                    nc.tensor.transpose(ps[:, 128 * (u * n + i) : 128 * (u * n + i) + 128], src, ident[:])
+            turned[s] = ps
 
-        def z_scale(w, n):
-            R = 128 * n
-            t = keep.tile([P, 4 * R], BF16, name="zgr%d" % w, align_bytes=64)
+        def z_scale(s):
+            rows = 128 * GROUP[s]
+            t = keep.tile([P, 4 * rows], BF16, name="z4_%d" % s, align_bytes=64)
             nc.vector.tensor_tensor(
                 out=t[:].rearrange("p (r u e) -> p r u e", u=2, e=2),
-                in0=X["zp", w][:, : 2 * R].bitcast(BF16).rearrange("p (u r e) -> p r u e", u=2, e=2),
-                in1=sc[:].rearrange("p (u e) -> p u e", u=2).unsqueeze(1).to_broadcast([P, R, 2, 2]),
+                in0=turned[s][:, : 2 * rows].bitcast(BF16).rearrange("p (u r e) -> p r u e", u=2, e=2),
+                in1=z_scales[:].rearrange("p (u e) -> p u e", u=2).unsqueeze(1).to_broadcast([P, rows, 2, 2]),
                 op=ALU.mult,
             )
-            X["zg", w] = t
+            z4[s] = t
 
-        def z_copy(w, n):
-            t = keep.tile([P, 512 * n], BF16, name="zgr%s" % w, align_bytes=64)
-            nc.scalar.copy(out=t[:].bitcast(F32).rearrange("p (r u) -> p r u", u=2), in_=X["zp", w][:, : 256 * n].rearrange("p (u r) -> p r u", u=2))
-            X["zg", w] = t
+        def z_copy(s):
+            rows = 128 * GROUP[s]
+            t = keep.tile([P, 4 * rows], BF16, name="z4_%s" % s, align_bytes=64)
+            nc.scalar.copy(out=t[:].bitcast(F32).rearrange("p (r u) -> p r u", u=2), in_=turned[s][:, : 2 * rows].rearrange("p (u r) -> p r u", u=2))
+            z4[s] = t
 
-        def z_quant(w, n):
-            c = keep.tile([P, 128 * n], U32, name="zc%s" % w, align_bytes=256)
-            s = keep.tile([P, 128 * n], U8, name="zs%s" % w, align_bytes=256)
-            nc.vector.quantize_mx(out=c[:].bitcast(FP8X4), scales=s[:], in_=X["zg", w][:])
-            for i in range(n):
-                X["z", w if w == "q" else w + i] = (c[:, 128 * i : 128 * i + 128], s[:, 128 * i : 128 * i + 128])
+        def z_quantise(s):
+            rows = 128 * GROUP[s]
+            codes = keep.tile([P, rows], U32, name="z_codes%s" % s, align_bytes=256)
+            scales = keep.tile([P, rows], U8, name="z_scale_bytes%s" % s, align_bytes=256)
+            nc.vector.quantize_mx(out=codes[:].bitcast(FP8X4), scales=scales[:], in_=z4[s][:])
+            for i in range(GROUP[s]):
+                c = slice(128 * i, 128 * i + 128)
+                z_mx[s if s == "q" else s + i] = (codes[:, c], scales[:, c])
 
-        def spread_turn():
-            ps = acc_tile(2)
-            for t in range(4):
-                nc.tensor.transpose(ps[:, 128 * t : 128 * t + 128], sc[:, t : t + 1].to_broadcast([P, P]), ident[:])
-            X["sp"] = ps
+        key_ps, value_ps, gate_ps = {}, {}, {}
+        neg_keys, bank_min, row_min, turned_min = {}, {}, {}, {}
 
-        def spread_copy():
-            nc.scalar.copy(out=scb[:].rearrange("p (m t) -> p m t", t=4), in_=X["sp"][:].rearrange("p (t m) -> p m t", t=4))
+        def key_mm(w, g):
+            key_ps[w, g] = bank()
+            mx(key_ps[w, g][:], z_mx[w], k_words, k_scales, 0, Q * g, Q)
 
-        def K_mm(w, g):
-            ps = rot_tile()
-            mm(ps[:], X["z", w], wk, kpl, 0, 512 * g, 512)
-            X["k", w, g] = ps
-
-        def K_copy(w, g):
-            if ("nk", w) not in X:
-                X["nk", w] = keep.tile([P, A], F32, name="nk%d" % (w % 3), tag="nk%d" % (w % 3))
-                X["mn", w] = work.tile([P, G], F32, name="mn", tag="mn")
+        def key_copy(w, g):
+            if g == 0:
+                neg_keys[w] = triple.tile([P, A], F32, name="neg_keys", tag="neg_keys")
+                bank_min[w] = pair.tile([P, G], F32, name="bank_min", tag="bank_min")
             nc.vector.tensor_scalar(
-                out=tm(X["nk", w][:, 512 * g : 512 * g + 512]),
-                in0=mt(X["k", w, g][:]),
+                out=grouped(neg_keys[w][:, Q * g : Q * g + Q]),
+                in0=natural(key_ps[w, g][:]),
                 scalar1=-1.0,
                 scalar2=None,
                 op0=ALU.mult,
                 op1=ALU.min,
-                accum_out=X["mn", w][:, g : g + 1],
+                accum_out=bank_min[w][:, g : g + 1],
             )
 
-        def M_v(w):
-            m1 = work.tile([P, 1], F32, name="m1", tag="m1")
-            nc.vector.tensor_reduce(out=m1[:], in_=X["mn", w][:], axis=AX.X, op=ALU.min)
-            X["m1", w] = m1
+        def row_minimum(w, part):
+            row_min[w] = pair.tile([P, 1], F32, name="row_min", tag="row_min")
+            nc.vector.tensor_reduce(out=row_min[w][:], in_=bank_min[w][:], axis=AX.X, op=ALU.min)
 
-        def M_pe(w):
-            ps = misc_tile()
-            nc.tensor.transpose(ps[:, 0:128], X["m1", w][:].to_broadcast([P, P]), ident[:])
-            X["m", w] = ps
+        def turn_minimum(w, part):
+            turned_min[w] = bank()
+            nc.tensor.transpose(turned_min[w][:, 0:P], row_min[w][:].to_broadcast([P, P]), ident[:])
 
-        def M_b(w):
-            nc.vector.tensor_reduce(out=nm[:, w : w + 1], in_=X["m", w][:, 0:128], axis=AX.X, op=ALU.min)
+        def step_minimum(w, part):
+            nc.vector.tensor_reduce(out=shift[:, w : w + 1], in_=turned_min[w][:, 0:P], axis=AX.X, op=ALU.min)
 
-        def E(w, i, parts):
-            if ("e", w) not in X:
-                X["e", w] = keep.tile([P, A], F32, name="e%d" % w)
-            n = A // parts
-            nc.scalar.activation(out=X["e", w][:, n * i : n * i + n], in_=X["nk", w][:, n * i : n * i + n], func=ACT.Exp, bias=nm[:, w : w + 1], scale=-1.0)
+        def exponential(w, half):
+            c = slice(1024 * half, 1024 * half + 1024)
+            nc.scalar.activation(out=weights[w][:, c], in_=neg_keys[w][:, c], func=ACT.Exp, bias=shift[:, w : w + 1], scale=-1.0)
 
-        def D(w, c0=0, c1=A):
+        def add_weights(engine, w, c0, c1):
             c = slice(c0, c1)
-            nc.gpsimd.tensor_tensor(out=den[:, c], in0=X["e", 0][:, c] if w == 1 else den[:, c], in1=X["e", w][:, c], op=ALU.add)
+            engine.tensor_tensor(out=den[:, c], in0=weights[0][:, c] if w == 1 else den[:, c], in1=weights[w][:, c], op=ALU.add)
 
-        num = [None] * G
+        def add_denominator(w, part):
+            if w == 6:
+                add_weights(nc.gpsimd, w, 0, 1024)
+                add_weights(nc.gpsimd, w, 1024, 2048)
+            elif w in VECTOR_HELPS:
+                add_weights(nc.gpsimd, w, 0, 1536)
+                add_weights(nc.vector, w, 1536, A)
+            elif 0 < w < 6:
+                add_weights(nc.gpsimd, w, 0, A)
 
-        def P_mm(w, g):
-            ps = rot_tile()
-            mm(ps[:], X["z", w], wv, vpl, 0, 512 * g, 512)
-            X["v", w, g] = ps
+        weighed, total = {}, {}
 
-        def P_v(w, g):
-            t = (late_pool if g == 3 else work).tile([P, 512], F32, name="ev%d" % g, tag="ev%d" % g)
-            nc.vector.tensor_tensor(out=tm(t[:]), in0=tm(X["e", w][:, 512 * g : 512 * g + 512]), in1=mt(X["v", w, g][:]), op=ALU.mult)
-            X["ev", w, g] = t
+        def value_mm(w, g):
+            value_ps[w, g] = bank()
+            mx(value_ps[w, g][:], z_mx[w], v_words, v_scales, 0, Q * g, Q)
 
-        def P_s(w, g):
-            v = work.tile([P, 512], F32, name="vs", tag="vs")
-            nc.scalar.copy(out=tm(v[:]), in_=mt(X["v", w, g][:]))
-            X["vs", w, g] = v
+        def weigh(w, g):
+            t = pair.tile([P, Q], F32, name="weighed%d" % g, tag="weighed%d" % g)
+            nc.vector.tensor_tensor(out=grouped(t[:]), in0=grouped(weights[w][:, Q * g : Q * g + Q]), in1=natural(value_ps[w, g][:]), op=ALU.mult)
+            weighed[w, g] = t
 
-        def P_g(w, g):
-            t = (late_pool if g == 3 else work).tile([P, 512], F32, name="ev%d" % g, tag="ev%d" % g)
-            nc.gpsimd.tensor_tensor(out=t[:], in0=X["e", w][:, 512 * g : 512 * g + 512], in1=X["vs", w, g][:], op=ALU.mult)
-            X["ev", w, g] = t
-
-        def T(w, g):
+        def add_turned(w, g):
             if w == 0:
-                num[g] = num_pool.tile([P, 512], F32, name="n%d" % (g % 3), tag="n%d" % (g % 3))
+                total[g] = sum_bank(g)
             for t in range(4):
                 c = slice(128 * t, 128 * t + 128)
-                nc.tensor.matmul(num[g][:, c], lhsT=X["ev", w, g][:, c], rhs=ident[:], start=(w == 0 and t == 0), stop=(w == W - 1 and t == 3), is_transpose=True)
+                nc.tensor.matmul(total[g][:, c], lhsT=weighed[w, g][:, c], rhs=ident[:], start=(w == 0 and t == 0), stop=(w == W - 1 and t == 3), is_transpose=True)
 
-        def q_turn():
-            ps = acc_tile(1)
-            words = zq_in[:].bitcast(F32)
-            for u in range(2):
-                nc.tensor.transpose(ps[:, u * 128 : u * 128 + 128], words[:, u : 256 : 2], ident[:])
-            X["zp", "q"] = ps
+        def gate_mm(g, part):
+            gate_ps[g] = bank()
+            mx(gate_ps[g][:], z_mx["q"], q_words, qo_scales, q_row, Q * g, Q)
 
-        def q_mm(g):
-            ps = rot_tile()
-            mm(ps[:], X["z", "q"], wq, vpl, 4, 512 * g, 512)
-            X["q", g] = ps
+        def gate_exp(g, part):
+            nc.scalar.activation(out=grouped(exp_q[:, Q * g : Q * g + Q]), in_=natural(gate_ps[g][:]), func=ACT.Exp, scale=-1.0)
 
-        def q_tanh(g):
-            nc.scalar.activation(out=tm(tq[:, 512 * g : 512 * g + 512]), in_=mt(X["q", g][:]), func=ACT.Tanh, scale=0.5)
+        def gate_plus_one(g, part):
+            c = slice(Q * g, Q * g + Q)
+            nc.scalar.activation(out=gate_den[:, c], in_=exp_q[:, c], func=ACT.Copy, bias=1.0)
 
-        def q_T(g):
-            ps = misc_tile()
+        divisor, turned_div, root, recip, h, h_mx, out_ps = {}, {}, {}, {}, {}, {}, {}
+
+        def div_multiply(g):
+            c = slice(Q * g, Q * g + Q)
+            divisor[g] = keep.tile([P, Q], F32, name="divisor%d" % g)
+            nc.vector.scalar_tensor_tensor(out=divisor[g][:], in0=den[:, c], scalar=EPS, in1=gate_den[:, c], op0=ALU.add, op1=ALU.mult)
+
+        def div_turn(g):
+            turned_div[g] = bank()
             for t in range(4):
                 c = slice(128 * t, 128 * t + 128)
-                nc.tensor.transpose(ps[:, c], tq[:, 512 * g + 128 * t : 512 * g + 128 * t + 128], ident[:])
-            X["qt", g] = ps
+                nc.tensor.transpose(turned_div[g][:, c], divisor[g][:, c], ident[:])
 
-        def q_out(g):
-            nc.scalar.activation(out=bt(tT[g][:]), in_=tb(X["qt", g][:]), func=ACT.Copy, bias=1.0)
+        def tokens_then_t(ap):
+            return ap.rearrange("p (t b) -> p b t", t=4)
 
-        def D_T(g):
-            ps = misc_tile()
-            srcs = [den] + [X["e", w] for w in PE_DEN]
-            for i in range(len(srcs)):
-                for t in range(4):
-                    c0 = 512 * g + 128 * t
-                    nc.tensor.matmul(ps[:, 128 * t : 128 * t + 128], lhsT=srcs[i][:, c0 : c0 + 128], rhs=ident[:], start=(i == 0 and t == 0), stop=(i == len(srcs) - 1 and t == 3), is_transpose=True)
-            X["d", g] = ps
+        def div_root(g):
+            root[g] = pair.tile([P, Q], F32, name="root", tag="root")
+            nc.scalar.activation(out=root[g][:].rearrange("p (b t) -> p b t", t=4), in_=tokens_then_t(turned_div[g][:]), func=ACT.Abs_reciprocal_sqrt)
 
-        def root(g):
-            s = work.tile([P, 512], F32, name="rs", tag="rs")
-            nc.scalar.activation(out=bt(s[:]), in_=tb(X["d", g][:]), func=ACT.Abs_reciprocal_sqrt, bias=2.0 * EPS, scale=2.0)
-            X["s", g] = s
+        def div_square(g):
+            recip[g] = pair.tile([P, Q], F32, name="recip", tag="recip")
+            nc.scalar.activation(out=recip[g][:], in_=root[g][:], func=ACT.Square)
 
-        def sq(g, vec=False):
-            r = work.tile([P, 512], F32, name="rr", tag="rr")
-            if vec:
-                nc.vector.tensor_tensor(out=r[:], in0=X["s", g][:], in1=X["s", g][:], op=ALU.mult)
-            else:
-                nc.scalar.activation(out=r[:], in_=X["s", g][:], func=ACT.Square)
-            X["r", g] = r
+        def h_multiply(g):
+            h[g] = pair.tile([P, Q], BF16, name="h", tag="h", align_bytes=64)
+            nc.vector.tensor_tensor(out=h[g][:].rearrange("p (b t) -> p b t", t=4), in0=recip[g][:].rearrange("p (b t) -> p b t", t=4), in1=tokens_then_t(total[g][:]), op=ALU.mult)
 
-        def n2(g):
-            t = work.tile([P, 512], F32, name="n2", tag="n2")
-            nc.vector.tensor_tensor(out=bt(t[:]), in0=bt(tT[g][:]), in1=tb(num[g][:]), op=ALU.mult)
-            X["n", g] = t
+        def h_quantise(g):
+            codes = keep.tile([P, B], U32, name="h_codes%d" % g, align_bytes=64)
+            scales = keep.tile([P, B], U8, name="h_scales%d" % g, align_bytes=64)
+            nc.vector.quantize_mx(out=codes[:].bitcast(FP8X4), scales=scales[:], in_=h[g][:])
+            h_mx[g] = (codes[:], scales[:])
 
-        def h_v(g):
-            t = work.tile([P, 512], BF16, name="hh", tag="hh", align_bytes=64)
-            nc.vector.tensor_tensor(out=t[:], in0=X["n", g][:], in1=X["r", g][:], op=ALU.mult)
-            X["h", g] = t
-
-        def h_q(g):
-            c = keep.tile([P, 128], U32, name="hc%d" % g, align_bytes=64)
-            s = keep.tile([P, 128], U8, name="hs%d" % g, align_bytes=64)
-            nc.vector.quantize_mx(out=c[:].bitcast(FP8X4), scales=s[:], in_=X["h", g][:])
-            X["hc", g] = (c[:], s[:])
-
-        def o_mm(g, i):
+        def out_mm(g, half):
             if g == 0:
-                X["o", i] = num_pool.tile([P, 512], F32, name="n%d" % (1 + i), tag="n%d" % (1 + i))
-            mm(X["o", i][:, 0:256], X["hc", g], wo, vpl, 8, 512 * g + 256 * i, 256, start=(g == 0), stop=(g == G - 1))
+                out_ps[half] = sum_bank(half)
+            mx(out_ps[half][:, 0:256], h_mx[g], o_words, qo_scales, o_row, Q * g + 256 * half, 256, start=(g == 0), stop=(g == G - 1))
 
-        o_sb = [keep.tile([P, 256], F32, name="o_sb%d" % i) for i in range(2)]
-
-        def o_out(i):
-            if i == 0:
-                nc.vector.tensor_copy(out=o_sb[i][:], in_=X["o", i][:, 0:256])
+        def out_store(half):
+            t = keep.tile([P, 256], F32, name="out%d" % half)
+            if half == 0:
+                nc.vector.tensor_copy(out=t[:], in_=out_ps[half][:, 0:256])
             else:
-                nc.scalar.copy(out=o_sb[i][:], in_=X["o", i][:, 0:256])
-            nc.sync.dma_start(out=out[:, 256 * i : 256 * i + 256], in_=o_sb[i][:])
+                nc.scalar.copy(out=t[:], in_=out_ps[half][:, 0:256])
+            nc.sync.dma_start(out=out[:, 256 * half : 256 * half + 256], in_=t[:])
 
-        seq = PARAM.get("order", "k0 k1 a0 k2 a1 k3 q0 a2 k4 q1 a3 k5 q2 a4 k6 q3 a5 k7 a6 b0 b1 a7 b2 b3 b4 b5 b6 b7").split()
-        gset = [tuple(u) for u in PARAM.get("gset", ())]
-        flat = []
-        for o in seq:
-            if o[0] == "q":
-                flat.append(("q", 0, int(o[1])))
-            else:
-                for g in {"k": (0, 1, 2, 3), "a": (0, 1, 2), "b": (3,)}[o[0]]:
-                    flat.append(("k" if o[0] == "k" else "p", int(o[1]), g))
-        idx = {flat[i]: i for i in range(len(flat))}
-        acts = []
+        z_calls = {"z_widen": z_widen, "z_multiply": z_multiply, "z_turn": z_turn, "z_scale": z_scale, "z_copy": z_copy, "z_quantise": z_quantise}
+        step_calls = {
+            "key_mm": key_mm,
+            "key_copy": key_copy,
+            "row_minimum": row_minimum,
+            "turn_minimum": turn_minimum,
+            "step_minimum": step_minimum,
+            "exponential": exponential,
+            "add_denominator": add_denominator,
+            "value_mm": value_mm,
+            "weigh": weigh,
+            "add_turned": add_turned,
+        }
+        gate_calls = {"gate_mm": gate_mm, "gate_exp": gate_exp, "gate_plus_one": gate_plus_one}
 
-        def at(name, pos, fn, *args):
-            if "log" in PARAM:
-                PARAM["log"][name] = pos
-            acts.append((PARAM.get(name, pos), len(acts), fn, args, name))
+        z_widen(1)
+        z_widen(0)
+        z_turn(0)
+        z_scale(0)
+        turn_scales()
+        z_quantise(0)
 
-        LK = PARAM.get("look", 3)
-        for i in range(len(flat)):
-            kind, w, g = flat[i]
-            fill = {"k": (K_mm, w, g), "p": (P_mm, w, g), "q": (q_mm, g)}[kind]
-            at("fill%d" % i, i - LK - 0.5, *fill)
-            if kind == "k":
-                at("use%d" % i, i, K_copy, w, g)
-            elif kind == "q":
-                at("use%d" % i, i, q_tanh, g)
-            elif (w, g) in gset:
-                at("vs%d_%d" % (w, g), i, P_s, w, g)
-                at("vg%d_%d" % (w, g), i, P_g, w, g)
-            else:
-                at("use%d" % i, i, P_v, w, g)
-        kb = [idx["k", w, 0] for w in range(W)]
+        for turn in range(TURNS):
+            for call, part, lag in TURN:
+                for name, s in PREPARE.get((turn, call, part), ()):
+                    z_calls[name](s)
+                i = turn - lag
+                if call in gate_calls and 0 <= i < G:
+                    gate_calls[call](i, part)
+                elif call in step_calls and 0 <= i < W:
+                    step_calls[call](i, part)
 
-        at("zw0", -9.0, z_widen, 0, 1, True)
-        at("zt0", -8.9, z_turn, 0, 1)
-        at("zw1", -8.8, z_widen, 1, 1)
-        at("zs0", -8.7, z_scale, 0, 1)
-        at("zq0", -8.4, z_quant, 0, 1)
-        if len(ZV) < 4:
-            at("spt", -8.3, spread_turn)
-            at("spc", -8.2, spread_copy)
-        for w, n, p0, p1, p2, p3 in ((1, 1, -8.6, -1.4, 0.05, 0.1), (2, 2, -4.1, 0.6, 2.1, 3.1), (4, 2, -3.0, 3.6, 4.1, 6.1), (6, 2, -2.9, 7.6, 8.1, 9.1)):
-            if w > 1:
-                at("zw%d" % w, p0 - 0.1, z_widen, w, n)
-            if w not in ZV:
-                at("zm%d" % w, p0, z_mul, w, n)
-            at("zt%d" % w, p1, z_turn, w, n)
-            at("zc%d" % w, p2 if w != 1 else 0.05, z_scale if w in ZV else z_copy, w, n)
-            at("zq%d" % w, p3, z_quant, w, n)
-        at("ztq", kb[2] + 0.1, q_turn)
-        at("zcq", kb[2] + 0.2, z_copy, "q", 1)
-        at("zqq", kb[2] + 1.2, z_quant, "q", 1)
-        p0 = [idx["k", 1, 0]] + [idx["p", w - 1, 0] for w in range(1, W)]
-        oM = PARAM.get("oM", (0.1, 1.1))
-        oR = PARAM.get("oR", (0.2, 0.2, 0.2, 0.2, 0.2, 0.2, 0.2, 0.2, 0.2, 3.2))
-        run = {}
-        for w in range(W):
-            b = p0[w]
-            x = b + oR[w]
-            at("mv%d" % w, b + oM[0], M_v, w)
-            run[w] = [("mp%d" % w, M_pe, w)]
-            at("mb%d" % w, b + oM[1], M_b, w)
-            for i in range(2):
-                at("e%d_%d" % (w, i), b + oM[1] + 0.01 + 0.01 * i, E, w, i, 2)
-            if w >= 1 and w not in PE_DEN:
-                if w < W - 1:
-                    at("d%d" % w, b + oM[1] + 0.05, D, w)
-                else:
-                    for i in range(4):
-                        at("d7_%d" % i, b + oM[1] + 0.05 + 0.01 * i, D, w, 512 * i, 512 * i + 512)
-        at("tab", p0[7] + oM[1] + 0.1, nc.scalar.activation, dummy[:], one[:], ACT.Abs_reciprocal_sqrt)
-        for g in range(G):
-            w = PARAM.get("qrun", (4, 5, 6, 7))[g]
-            run[w] += [("qt%d" % g, q_T, g), ("qo%d" % g, q_out, g)]
-        run[8] = []
-        run[9] = []
-        for w in range(W):
-            for g in range(3):
-                run[w + 2] += [("t%d_%d" % (w, g), T, w, g)]
-        p0 += [idx["p", 7, 0], idx["p", 7, 2]]
-        for w in range(10):
-            for j in range(len(run[w])):
-                at(run[w][j][0], p0[w] + oR[w] + 0.001 * j, *run[w][j][1:])
-        oL = PARAM.get("oL", (0.5, 3.5))
-        for w in range(W):
-            at("t%d_3" % w, max(idx["p", w, 3] + 1.4, p0[9] + oR[9] + oL[0] + (oL[1] if w > PARAM.get("oLw", 3) else 0)) + 0.001 * w, T, w, 3)
-        n = len(flat)
-        e0 = p0[9] + oR[9]
-        for g in range(G):
-            r = PARAM.get("oDT", (p0[8] + 0.3, p0[8] + 1.3, p0[9] + 2.3, p0[9] + 4.3))[g]
-            at("dt%d" % g, r, D_T, g)
-            at("ro%d" % g, r + 0.001, root, g)
-            at("sq%d" % g, r + 0.002, sq, g)
-            b = e0 + PARAM.get("oN2", 0.05) + g * 1.0 if g < 3 else n + 4
-            at("n2_%d" % g, b, n2, g)
-            at("h%d" % g, b + PARAM.get("oH", 1.0), h_v, g)
-            at("hq%d" % g, b + PARAM.get("oH", 1.0) + 1.0, h_q, g)
-            for i in range(2):
-                at("om%d_%d" % (g, i), max(b + PARAM.get("oH", 1.0) + 1.1, e0 + 4.5 + 0.1 * g) + 0.01 * i, o_mm, g, i)
-        for i in range(2):
-            at("oo%d" % i, n + 20 + i, o_out, i)
-        acts.sort(key=lambda a: (a[0], a[1]))
-        for a in acts:
-            if "marks" in PARAM:
-                PARAM["marks"].append((a[4], PARAM["cnt"]()))
-            a[2](*a[3])
+        nc.scalar.activation(out=table[:], in_=one[:], func=ACT.Abs_reciprocal_sqrt)
+
+        def last_weights(g):
+            add_weights(nc.vector, W - 1, Q * g, Q * g + Q)
+
+        last_weights(0)
+        last_weights(1)
+        div_multiply(0)
+        div_multiply(1)
+        div_turn(0)
+        last_weights(3)
+        div_turn(1)
+        value_mm(7, 2)
+        last_weights(2)
+        div_root(0)
+        weigh(7, 3)
+        div_multiply(2)
+        div_multiply(3)
+        weigh(7, 2)
+        div_root(1)
+        add_turned(6, 3)
+        add_turned(7, 1)
+        div_square(0)
+        div_square(1)
+        h_multiply(0)
+        div_turn(2)
+        div_turn(3)
+        h_multiply(1)
+        add_turned(7, 2)
+        h_quantise(0)
+        div_root(2)
+        h_quantise(1)
+        add_turned(7, 3)
+        div_root(3)
+        div_square(2)
+        h_multiply(2)
+        out_mm(0, 1)
+        div_square(3)
+        h_multiply(3)
+        h_quantise(2)
+        out_mm(1, 1)
+        out_mm(0, 0)
+        h_quantise(3)
+        out_mm(1, 0)
+        out_mm(2, 1)
+        out_mm(3, 1)
+        out_mm(2, 0)
+        out_mm(3, 0)
+        out_store(1)
+        out_store(0)

from contextlib import ExitStack

import concourse.mybir as mybir
from concourse.masks import make_identity

F32 = mybir.dt.float32
BF16 = mybir.dt.bfloat16
I32 = mybir.dt.int32
U32 = mybir.dt.uint32
U8 = mybir.dt.uint8
FP8 = mybir.dt.float8_e4m3fn
FP8X4 = mybir.dt.float8_e4m3fn_x4
ACT = mybir.ActivationFunctionType
ALU = mybir.AluOpType
AX = mybir.AxisListType

P = 128
B, L, A, W = 128, 512, 2048, 8
Q = 512
G = A // Q
EPS = 1e-8
FLOPS = 2 * B * L * A * (1 + 2 * W) + 2 * B * A * L

WINDOW_CUTS = (0, 1, 4, 8)

TURN = (
    ("value_mm", 2, 2),
    ("exponential", 0, 1),
    ("key_mm", 0, 0),
    ("weigh", 3, 2),
    ("key_mm", 1, 0),
    ("key_mm", 3, 0),
    ("weigh", 2, 2),
    ("key_copy", 0, 0),
    ("gate_mm", 0, 3),
    ("add_turned", 3, 3),
    ("add_turned", 1, 2),
    ("add_denominator", 0, 2),
    ("exponential", 1, 1),
    ("key_copy", 1, 0),
    ("key_mm", 2, 0),
    ("value_mm", 0, 1),
    ("gate_exp", 0, 3),
    ("gate_plus_one", 0, 4),
    ("value_mm", 1, 1),
    ("value_mm", 3, 1),
    ("key_copy", 3, 0),
    ("key_copy", 2, 0),
    ("weigh", 0, 1),
    ("row_minimum", 0, 0),
    ("weigh", 1, 1),
    ("add_turned", 2, 2),
    ("turn_minimum", 0, 0),
    ("add_turned", 0, 1),
    ("step_minimum", 0, 0),
)
TURNS = W + 1

PREPARE = {
    (0, "key_mm", 1): (("z_widen", 2), ("z_turn", 1)),
    (0, "key_copy", 1): (("z_scale", 1),),
    (0, "value_mm", 0): (("z_turn", 2), ("z_widen", 6)),
    (0, "gate_exp", 0): (("z_quantise", 1),),
    (0, "turn_minimum", 0): (("z_scale", 2),),
    (1, "key_mm", 0): (("z_widen", 4),),
    (1, "value_mm", 3): (("z_turn", "q"), ("z_multiply", 6)),
    (1, "key_copy", 2): (("z_quantise", 2), ("z_turn", 6)),
    (1, "turn_minimum", 0): (("z_copy", "q"),),
    (2, "key_copy", 0): (("z_multiply", 4),),
    (2, "add_turned", 3): (("z_quantise", "q"),),
    (2, "add_denominator", 0): (("z_turn", 4),),
    (2, "value_mm", 0): (("z_copy", 4),),
    (3, "add_denominator", 0): (("z_copy", 6),),
    (3, "gate_plus_one", 0): (("z_quantise", 6), ("z_quantise", 4)),
}
GROUP = {0: 1, 1: 1, 2: 2, 4: 2, 6: 2, "q": 1}
SCALED_LATE = (0, 1, 2)
VECTOR_HELPS = (2, 4)
TURNED_IN = {0: 3, 1: 0, 2: 1, 4: 2, 6: 3, "q": 0}


def grouped(ap):
    return ap.rearrange("p (t m) -> p t m", t=4)


def natural(ap):
    return ap.rearrange("p (m t) -> p t m", t=4)


def tile_aftblock_pa_w8_kernel(tc, z_current, z_window_bytes, z_window_scale, Wq_words, Wq_scales, Wk_words, Wk_scales, Wv_words, Wv_scales, Wo_words, Wo_scales, out):
    nc = tc.nc
    with ExitStack() as ctx:
        keep = ctx.enter_context(tc.tile_pool(name="keep", bufs=1))
        pair = ctx.enter_context(tc.tile_pool(name="pair", bufs=2))
        triple = ctx.enter_context(tc.tile_pool(name="triple", bufs=3))
        sum_pool = ctx.enter_context(tc.psum_pool(name="sums", bufs=1))
        bank_pool = ctx.enter_context(tc.psum_pool(name="banks", bufs=4))
        ctx.enter_context(tc.manual_schedule())

        def sum_bank(i):
            return sum_pool.tile([P, Q], F32, name="sum%d" % i, tag="sum%d" % i)

        def bank():
            return bank_pool.tile([P, Q], F32, name="bank", tag="bank")

        ident = keep.tile([P, P], F32, name="ident")
        one = keep.tile([P, 1], F32, name="one")
        table = keep.tile([P, 1], F32, name="table")

        k_words = keep.tile([P, A], U32, name="k_words", align_bytes=256)
        v_words = keep.tile([P, A], U32, name="v_words", align_bytes=256)
        q_words = keep.tile([P, A], U32, name="q_words", align_bytes=256)
        o_words = keep.tile([P, A], U32, name="o_words", align_bytes=256)
        k_scales = keep.tile([P, A], U8, name="k_scales", align_bytes=256)
        v_scales = keep.tile([P, A], U8, name="v_scales", align_bytes=256)
        qo_scales = keep.tile([P, A], U8, name="qo_scales", align_bytes=256)
        q_row, o_row = 0, 4

        z_bytes = [keep.tile([P, WINDOW_CUTS[i + 1] - WINDOW_CUTS[i], L], U8, name="z_bytes%d" % i, align_bytes=64) for i in range(3)]
        zc = keep.tile([P, L], BF16, name="zc", align_bytes=64)
        z_scales = keep.tile([P, 4], F32, name="z_scales")
        z_scales_wide = keep.tile([P, L], F32, name="z_scales_wide")

        weights = [keep.tile([P, A], F32, name="weights%d" % w) for w in range(W)]
        shift = keep.tile([P, W], F32, name="shift")
        den = keep.tile([P, A], F32, name="den")
        exp_q = keep.tile([P, A], F32, name="exp_q")
        gate_den = keep.tile([P, A], F32, name="gate_den")

        nc.vector.memset(k_scales[:].bitcast(U32), 0)
        nc.vector.memset(one[:], 1.0)
        nc.vector.memset(v_scales[:].bitcast(U32), 0)
        make_identity(nc, ident[:])
        nc.gpsimd.memset(qo_scales[:].bitcast(U32), 0)

        def load_window(i):
            nc.sync.dma_start(out=z_bytes[i][:], in_=z_window_bytes[WINDOW_CUTS[i] : WINDOW_CUTS[i + 1]].rearrange("w b k -> b w k"))

        def load_scales(tile, row, src):
            for r in range(4):
                nc.sync.dma_start(out=tile[32 * r + row : 32 * r + row + 4, :].bitcast(I32), in_=src[4 * r : 4 * r + 4, :].bitcast(I32))

        def load_words(tile, src, c0, c1):
            nc.sync.dma_start(out=tile[:, c0:c1].bitcast(I32), in_=src.rearrange("p n t -> p (n t)")[:, 4 * c0 : 4 * c1].bitcast(I32))

        nc.sync.dma_start(out=z_scales[:], in_=z_window_scale.rearrange("o c (p t) -> p (o c t)", t=4))
        load_window(0)
        load_scales(k_scales, 0, Wk_scales[0])
        load_words(k_words, Wk_words[0], 0, 512)
        load_window(1)
        load_words(k_words, Wk_words[0], 512, 1024)
        load_words(k_words, Wk_words[0], 1024, 2048)
        load_window(2)
        load_scales(v_scales, 0, Wv_scales[0])
        for half in (0, 1024):
            load_words(v_words, Wv_words[0], half, half + 1024)
        nc.sync.dma_start(out=zc[:], in_=z_current)
        load_scales(qo_scales, q_row, Wq_scales[0])
        for half in (0, 1024):
            load_words(q_words, Wq_words[0], half, half + 1024)
        for r in range(4):
            nc.sync.dma_start(
                out=qo_scales[32 * r + o_row : 32 * r + o_row + 4, :].bitcast(I32).rearrange("p (g n) -> p g n", g=G),
                in_=Wo_scales.bitcast(I32)[:, 4 * r : 4 * r + 4, :].rearrange("g q n -> q g n"),
            )
        nc.sync.dma_start(out=o_words[:].bitcast(I32).rearrange("p (g n) -> p g n", g=G), in_=Wo_words.rearrange("g p n t -> p g (n t)").bitcast(I32))

        nc.scalar.activation(out=table[:], in_=one[:], func=ACT.Exp)

        def mx(ps, stationary, words, scales, row, c0, n, start=True, stop=True):
            codes, bytes_of_codes = stationary
            nc.tensor.matmul_mx(
                out=ps,
                lhsT=codes.bitcast(FP8X4),
                lhsT_scale=bytes_of_codes,
                rhs=words[:, c0 : c0 + n].bitcast(FP8X4),
                rhs_scale=scales[row:P, c0 : c0 + n],
                start=start,
                stop=stop,
            )

        wide = {}
        turned = {}
        z4 = {}
        z_mx = {}
        wide["q"] = zc[:].unsqueeze(1)

        def z_widen(s):
            n = GROUP[s]
            t = keep.tile([P, n, L], BF16, name="wide%d" % s, align_bytes=64)
            i = max(i for i in range(3) if WINDOW_CUTS[i] <= s)
            src = z_bytes[i][:, s - WINDOW_CUTS[i] : s - WINDOW_CUTS[i] + n, :].bitcast(FP8)
            if s == 0:
                nc.vector.tensor_copy(out=t[:], in_=src)
            else:
                nc.scalar.copy(out=t[:], in_=src)
            wide[s] = t

        def turn_scales():
            ps = sum_bank(2)
            for t in range(4):
                nc.tensor.transpose(ps[:, 128 * t : 128 * t + 128], z_scales[:, t : t + 1].to_broadcast([P, P]), ident[:])
            nc.scalar.copy(out=z_scales_wide[:].rearrange("p (u m e) -> p u m e", u=2, e=2), in_=ps[:].rearrange("p (u e m) -> p u m e", u=2, e=2))

        def z_multiply(s):
            t = keep.tile([P, GROUP[s], L], BF16, name="product%d" % s, align_bytes=64)
            for i in range(GROUP[s]):
                nc.gpsimd.tensor_tensor(
                    out=t[:, i, :].rearrange("p (u m e) -> p u m e", u=2, e=2),
                    in0=wide[s][:, i, :].rearrange("p (m u e) -> p u m e", u=2, e=2),
                    in1=z_scales_wide[:].rearrange("p (u m e) -> p u m e", u=2, e=2),
                    op=ALU.mult,
                )
            wide[s] = t

        def z_turn(s):
            n = GROUP[s]
            ps = sum_bank(TURNED_IN[s])
            for i in range(n):
                words = wide[s][:, i, :].bitcast(F32)
                for u in range(2):
                    src = words[:, u:256:2] if s == "q" or s in SCALED_LATE else words[:, 128 * u : 128 * u + 128]
                    nc.tensor.transpose(ps[:, 128 * (u * n + i) : 128 * (u * n + i) + 128], src, ident[:])
            turned[s] = ps

        def z_scale(s):
            rows = 128 * GROUP[s]
            t = keep.tile([P, 4 * rows], BF16, name="z4_%d" % s, align_bytes=64)
            nc.vector.tensor_tensor(
                out=t[:].rearrange("p (r u e) -> p r u e", u=2, e=2),
                in0=turned[s][:, : 2 * rows].bitcast(BF16).rearrange("p (u r e) -> p r u e", u=2, e=2),
                in1=z_scales[:].rearrange("p (u e) -> p u e", u=2).unsqueeze(1).to_broadcast([P, rows, 2, 2]),
                op=ALU.mult,
            )
            z4[s] = t

        def z_copy(s):
            rows = 128 * GROUP[s]
            t = keep.tile([P, 4 * rows], BF16, name="z4_%s" % s, align_bytes=64)
            nc.scalar.copy(out=t[:].bitcast(F32).rearrange("p (r u) -> p r u", u=2), in_=turned[s][:, : 2 * rows].rearrange("p (u r) -> p r u", u=2))
            z4[s] = t

        def z_quantise(s):
            rows = 128 * GROUP[s]
            codes = keep.tile([P, rows], U32, name="z_codes%s" % s, align_bytes=256)
            scales = keep.tile([P, rows], U8, name="z_scale_bytes%s" % s, align_bytes=256)
            nc.vector.quantize_mx(out=codes[:].bitcast(FP8X4), scales=scales[:], in_=z4[s][:])
            for i in range(GROUP[s]):
                c = slice(128 * i, 128 * i + 128)
                z_mx[s if s == "q" else s + i] = (codes[:, c], scales[:, c])

        key_ps, value_ps, gate_ps = {}, {}, {}
        neg_keys, bank_min, row_min, turned_min = {}, {}, {}, {}

        def key_mm(w, g):
            key_ps[w, g] = bank()
            mx(key_ps[w, g][:], z_mx[w], k_words, k_scales, 0, Q * g, Q)

        def key_copy(w, g):
            if g == 0:
                neg_keys[w] = triple.tile([P, A], F32, name="neg_keys", tag="neg_keys")
                bank_min[w] = pair.tile([P, G], F32, name="bank_min", tag="bank_min")
            nc.vector.tensor_scalar(
                out=grouped(neg_keys[w][:, Q * g : Q * g + Q]),
                in0=natural(key_ps[w, g][:]),
                scalar1=-1.0,
                scalar2=None,
                op0=ALU.mult,
                op1=ALU.min,
                accum_out=bank_min[w][:, g : g + 1],
            )

        def row_minimum(w, part):
            row_min[w] = pair.tile([P, 1], F32, name="row_min", tag="row_min")
            nc.vector.tensor_reduce(out=row_min[w][:], in_=bank_min[w][:], axis=AX.X, op=ALU.min)

        def turn_minimum(w, part):
            turned_min[w] = bank()
            nc.tensor.transpose(turned_min[w][:, 0:P], row_min[w][:].to_broadcast([P, P]), ident[:])

        def step_minimum(w, part):
            nc.vector.tensor_reduce(out=shift[:, w : w + 1], in_=turned_min[w][:, 0:P], axis=AX.X, op=ALU.min)

        def exponential(w, half):
            c = slice(1024 * half, 1024 * half + 1024)
            nc.scalar.activation(out=weights[w][:, c], in_=neg_keys[w][:, c], func=ACT.Exp, bias=shift[:, w : w + 1], scale=-1.0)

        def add_weights(engine, w, c0, c1):
            c = slice(c0, c1)
            engine.tensor_tensor(out=den[:, c], in0=weights[0][:, c] if w == 1 else den[:, c], in1=weights[w][:, c], op=ALU.add)

        def add_denominator(w, part):
            if w == 6:
                add_weights(nc.gpsimd, w, 0, 1024)
                add_weights(nc.gpsimd, w, 1024, 2048)
            elif w in VECTOR_HELPS:
                add_weights(nc.gpsimd, w, 0, 1536)
                add_weights(nc.vector, w, 1536, A)
            elif 0 < w < 6:
                add_weights(nc.gpsimd, w, 0, A)

        weighed, total = {}, {}

        def value_mm(w, g):
            value_ps[w, g] = bank()
            mx(value_ps[w, g][:], z_mx[w], v_words, v_scales, 0, Q * g, Q)

        def weigh(w, g):
            t = pair.tile([P, Q], F32, name="weighed%d" % g, tag="weighed%d" % g)
            nc.vector.tensor_tensor(out=grouped(t[:]), in0=grouped(weights[w][:, Q * g : Q * g + Q]), in1=natural(value_ps[w, g][:]), op=ALU.mult)
            weighed[w, g] = t

        def add_turned(w, g):
            if w == 0:
                total[g] = sum_bank(g)
            for t in range(4):
                c = slice(128 * t, 128 * t + 128)
                nc.tensor.matmul(total[g][:, c], lhsT=weighed[w, g][:, c], rhs=ident[:], start=(w == 0 and t == 0), stop=(w == W - 1 and t == 3), is_transpose=True)

        def gate_mm(g, part):
            gate_ps[g] = bank()
            mx(gate_ps[g][:], z_mx["q"], q_words, qo_scales, q_row, Q * g, Q)

        def gate_exp(g, part):
            nc.scalar.activation(out=grouped(exp_q[:, Q * g : Q * g + Q]), in_=natural(gate_ps[g][:]), func=ACT.Exp, scale=-1.0)

        def gate_plus_one(g, part):
            c = slice(Q * g, Q * g + Q)
            nc.scalar.activation(out=gate_den[:, c], in_=exp_q[:, c], func=ACT.Copy, bias=1.0)

        divisor, turned_div, root, recip, h, h_mx, out_ps = {}, {}, {}, {}, {}, {}, {}

        def div_multiply(g):
            c = slice(Q * g, Q * g + Q)
            divisor[g] = keep.tile([P, Q], F32, name="divisor%d" % g)
            nc.vector.scalar_tensor_tensor(out=divisor[g][:], in0=den[:, c], scalar=EPS, in1=gate_den[:, c], op0=ALU.add, op1=ALU.mult)

        def div_turn(g):
            turned_div[g] = bank()
            for t in range(4):
                c = slice(128 * t, 128 * t + 128)
                nc.tensor.transpose(turned_div[g][:, c], divisor[g][:, c], ident[:])

        def tokens_then_t(ap):
            return ap.rearrange("p (t b) -> p b t", t=4)

        def div_root(g):
            root[g] = pair.tile([P, Q], F32, name="root", tag="root")
            nc.scalar.activation(out=root[g][:].rearrange("p (b t) -> p b t", t=4), in_=tokens_then_t(turned_div[g][:]), func=ACT.Abs_reciprocal_sqrt)

        def div_square(g):
            recip[g] = pair.tile([P, Q], F32, name="recip", tag="recip")
            nc.scalar.activation(out=recip[g][:], in_=root[g][:], func=ACT.Square)

        def h_multiply(g):
            h[g] = pair.tile([P, Q], BF16, name="h", tag="h", align_bytes=64)
            nc.vector.tensor_tensor(out=h[g][:].rearrange("p (b t) -> p b t", t=4), in0=recip[g][:].rearrange("p (b t) -> p b t", t=4), in1=tokens_then_t(total[g][:]), op=ALU.mult)

        def h_quantise(g):
            codes = keep.tile([P, B], U32, name="h_codes%d" % g, align_bytes=64)
            scales = keep.tile([P, B], U8, name="h_scales%d" % g, align_bytes=64)
            nc.vector.quantize_mx(out=codes[:].bitcast(FP8X4), scales=scales[:], in_=h[g][:])
            h_mx[g] = (codes[:], scales[:])

        def out_mm(g, half):
            if g == 0:
                out_ps[half] = sum_bank(half)
            mx(out_ps[half][:, 0:256], h_mx[g], o_words, qo_scales, o_row, Q * g + 256 * half, 256, start=(g == 0), stop=(g == G - 1))

        def out_store(half):
            t = keep.tile([P, 256], F32, name="out%d" % half)
            if half == 0:
                nc.vector.tensor_copy(out=t[:], in_=out_ps[half][:, 0:256])
            else:
                nc.scalar.copy(out=t[:], in_=out_ps[half][:, 0:256])
            nc.sync.dma_start(out=out[:, 256 * half : 256 * half + 256], in_=t[:])

        z_calls = {"z_widen": z_widen, "z_multiply": z_multiply, "z_turn": z_turn, "z_scale": z_scale, "z_copy": z_copy, "z_quantise": z_quantise}
        step_calls = {
            "key_mm": key_mm,
            "key_copy": key_copy,
            "row_minimum": row_minimum,
            "turn_minimum": turn_minimum,
            "step_minimum": step_minimum,
            "exponential": exponential,
            "add_denominator": add_denominator,
            "value_mm": value_mm,
            "weigh": weigh,
            "add_turned": add_turned,
        }
        gate_calls = {"gate_mm": gate_mm, "gate_exp": gate_exp, "gate_plus_one": gate_plus_one}

        z_widen(1)
        z_widen(0)
        z_turn(0)
        z_scale(0)
        turn_scales()
        z_quantise(0)

        for turn in range(TURNS):
            for call, part, lag in TURN:
                for name, s in PREPARE.get((turn, call, part), ()):
                    z_calls[name](s)
                i = turn - lag
                if call in gate_calls and 0 <= i < G:
                    gate_calls[call](i, part)
                elif call in step_calls and 0 <= i < W:
                    step_calls[call](i, part)

        nc.scalar.activation(out=table[:], in_=one[:], func=ACT.Abs_reciprocal_sqrt)

        def last_weights(g):
            add_weights(nc.vector, W - 1, Q * g, Q * g + Q)

        last_weights(0)
        last_weights(1)
        div_multiply(0)
        div_multiply(1)
        div_turn(0)
        last_weights(3)
        div_turn(1)
        value_mm(7, 2)
        last_weights(2)
        div_root(0)
        weigh(7, 3)
        div_multiply(2)
        div_multiply(3)
        weigh(7, 2)
        div_root(1)
        add_turned(6, 3)
        add_turned(7, 1)
        div_square(0)
        div_square(1)
        h_multiply(0)
        div_turn(2)
        div_turn(3)
        h_multiply(1)
        add_turned(7, 2)
        h_quantise(0)
        div_root(2)
        h_quantise(1)
        add_turned(7, 3)
        div_root(3)
        div_square(2)
        h_multiply(2)
        out_mm(0, 1)
        div_square(3)
        h_multiply(3)
        h_quantise(2)
        out_mm(1, 1)
        out_mm(0, 0)
        h_quantise(3)
        out_mm(1, 0)
        out_mm(2, 1)
        out_mm(3, 1)
        out_mm(2, 0)
        out_mm(3, 0)
        out_store(1)
        out_store(0)
